import numpy as np
import ml_dtypes


def mxq(x, axis, fmt="e4m3"):
    dtype, down = {"e4m3": (ml_dtypes.float8_e4m3fn, 7), "e5m2": (ml_dtypes.float8_e5m2, 14)}[fmt]
    v = np.moveaxis(np.asarray(x, np.float32).astype(ml_dtypes.bfloat16).astype(np.float64), axis, -1)
    blocks = v.reshape(v.shape[:-1] + (-1, 32))
    amax = np.abs(blocks).max(-1, keepdims=True)
    byte = np.maximum(np.where(amax > 0, np.frexp(amax)[1] - 1 + 127, 0) - down, 1)
    scale = np.exp2(byte - 127.0)
    codes = (blocks / scale).astype(np.float32).astype(dtype).astype(np.float64)
    return np.moveaxis((codes * scale).reshape(v.shape), -1, axis)


WIDE = False


def mx_kscale(k):
    if not WIDE:
        return np.ones(k)
    levels = np.array([10, -10, 5, -5, 0])
    a = np.random.permutation(np.resize(levels, k // 512 * 4)).reshape(k // 512, 4)
    idx = np.arange(k)
    return np.exp2(a[idx // 512, idx % 128 // 32])


BF16 = ml_dtypes.bfloat16


def bf(x):
    return np.asarray(x, np.float32).astype(BF16)


def f64(x):
    return np.asarray(x).astype(np.float64)


E2M1 = np.array([0.0, 0.5, 1.0, 1.5, 2.0, 3.0, 4.0, 6.0, -0.0, -0.5, -1.0, -1.5, -2.0, -3.0, -4.0, -6.0])


def pack_weight(w, fmt):
    k, n = w.shape
    w = f64(bf(w)).reshape(k // 32, 32, n)
    amax = np.abs(w).max(1)
    if fmt == "e4m3":
        byte = np.frexp(amax)[1] - 1 + 127 - 7
    else:
        mant, ex = np.frexp(amax / 6.0)
        byte = np.where(mant > 0.5, ex, ex - 1) + 127
    byte = np.clip(np.where(amax > 0, byte, 1), 1, 254)
    scaled = (w * np.exp2(127.0 - byte)[:, None, :]).reshape(k, n).astype(np.float32)
    by_word = np.ascontiguousarray(scaled.reshape(k // 512, 128, 4, n).transpose(0, 1, 3, 2))
    if fmt == "e4m3":
        words = by_word.astype(ml_dtypes.float8_e4m3fn).view(np.uint8)
    else:
        c = by_word.astype(ml_dtypes.float4_e2m1fn).view(np.uint8) & 0xF
        words = c[..., 0::2] | (c[..., 1::2] << 4)
    return np.ascontiguousarray(words), np.ascontiguousarray(byte.astype(np.uint8).reshape(k // 512, 16, n))


def unpack_weight(words, scales, fmt):
    g, p, n, _ = words.shape
    if fmt == "e4m3":
        vals = np.ascontiguousarray(words).view(ml_dtypes.float8_e4m3fn).astype(np.float64)
    else:
        nib = np.empty((g, p, n, 4), np.uint8)
        nib[..., 0::2] = words & 0xF
        nib[..., 1::2] = words >> 4
        vals = E2M1[nib]
    vals = vals * np.repeat(np.exp2(scales.astype(np.float64) - 127.0), 8, axis=1)[..., None]
    return vals.transpose(0, 1, 3, 2).reshape(g * 512, n)


B, CH, C1, C2, D, NF, W, H = 2, 1024, 128, 256, 2, 16, 16, 16
N = NF * W * H
M = NF * (W // D) * (H // D)
FMT = "e4m3"


def conv(xq, w_words, w_scales, b):
    return (unpack_weight(w_words, w_scales, FMT).T @ xq) + f64(b)[None, :, None]


def maxpool_wh(v):
    return v.reshape(B, -1, NF, W // D, D, H // D, D).max(axis=(4, 6)).reshape(B, -1, M)


def setup_inputs():
    s = mx_kscale(CH)
    x = bf(np.random.standard_normal((B, CH, NF, W, H)) * s[None, :, None, None, None])
    w_theta = np.random.standard_normal((C1, CH)) * 0.3 / np.sqrt(CH) / s
    b_theta = bf(np.random.standard_normal(C1) * 0.1)
    w_phi = np.random.standard_normal((C1, CH)) * 0.3 / np.sqrt(CH) / s
    b_phi = bf(np.random.standard_normal(C1) * 0.1)
    w_g = np.random.standard_normal((C2, CH)) / np.sqrt(CH) / s
    b_g = bf(np.random.standard_normal(C2) * 0.2)
    w_theta_words, w_theta_scales = pack_weight(np.ascontiguousarray(w_theta.T), FMT)
    w_phi_words, w_phi_scales = pack_weight(np.ascontiguousarray(w_phi.T), FMT)
    w_g_words, w_g_scales = pack_weight(np.ascontiguousarray(w_g.T), FMT)
    return {"x": x,
            "w_theta_words": w_theta_words,
            "w_theta_scales": w_theta_scales,
            "b_theta": b_theta,
            "w_phi_words": w_phi_words,
            "w_phi_scales": w_phi_scales,
            "b_phi": b_phi,
            "w_g_words": w_g_words,
            "w_g_scales": w_g_scales,
            "b_g": b_g}


def reference(x, w_theta_words, w_theta_scales, b_theta, w_phi_words, w_phi_scales, b_phi, w_g_words, w_g_scales, b_g):
    xq = mxq(f64(x).reshape(B, CH, N), 1, "e4m3")
    theta = np.tanh(conv(xq, w_theta_words, w_theta_scales, b_theta)).transpose(0, 2, 1)
    phi = maxpool_wh(np.tanh(conv(xq, w_phi_words, w_phi_scales, b_phi))).transpose(0, 2, 1)
    g = maxpool_wh(conv(xq, w_g_words, w_g_scales, b_g)).transpose(0, 2, 1)
    return theta, phi, g

@@ -1,0 +1,231 @@
+from contextlib import ExitStack
+
+import concourse.mybir as mybir
+
+BF16 = mybir.dt.bfloat16
+F32 = mybir.dt.float32
+I32 = mybir.dt.int32
+U32 = mybir.dt.uint32
+U8 = mybir.dt.uint8
+FP8X4 = mybir.dt.float8_e4m3fn_x4
+ADD = mybir.AluOpType.add
+MAX = mybir.AluOpType.max
+TANH = mybir.ActivationFunctionType.Tanh
+
+P = 128
+PACK = 4
+K_PASS = P * PACK
+
+BATCH = 2
+CHANNELS = 1024
+PASSES = CHANNELS // K_PASS
+LOCATIONS = 16 * 16 * 16
+
+C_THETA = 128
+C_PHI = 128
+C_G = 256
+C_POOLED = C_PHI + C_G
+C_ALL = C_THETA + C_POOLED
+
+PAIRS = 32
+HALVES = 2
+QUADS = 4
+QUAD = 4
+WINDOWS = 2
+SIDES = 2
+CHUNK = PAIRS * HALVES * QUADS * QUAD
+CHUNKS = LOCATIONS // CHUNK
+POOLED_CHUNK = CHUNK // 4
+
+V_PAIRS = 12
+
+FLOPS = 2 * BATCH * LOCATIONS * CHANNELS * C_ALL
+
+assert PAIRS * QUADS == P
+assert WINDOWS * SIDES == QUAD
+
+
+def load_weights(nc, consts, weights):
+    w_words = consts.tile([P, PASSES, C_ALL], U32, align_bytes=64)
+    w_planes = consts.tile([P, PASSES, C_ALL], U8, align_bytes=64)
+    nc.vector.memset(w_planes[:].bitcast(I32), 0)
+    for words, scales, first, count in weights:
+        cols = slice(first, first + count)
+        nc.sync.dma_start(
+            out=w_words[:, :, cols].bitcast(I32),
+            in_=words.rearrange("g p n t -> p g (n t)").bitcast(I32),
+        )
+        for quadrant in range(4):
+            nc.sync.dma_start(
+                out=w_planes[32 * quadrant : 32 * quadrant + 4, :, cols].bitcast(I32),
+                in_=scales[:, 4 * quadrant : 4 * quadrant + 4, :].rearrange("g r n -> r g n").bitcast(I32),
+            )
+    return w_words, w_planes
+
+
+def spread_biases(nc, consts, psum, biases):
+    bias_rows = consts.tile([P, C_ALL], BF16)
+    ones = consts.tile([P, P], BF16)
+    nc.vector.memset(bias_rows[:], 0.0)
+    nc.vector.memset(ones[:], 1.0)
+    for bias, first, count in biases:
+        nc.scalar.dma_start(
+            out=bias_rows[0:1, first : first + count],
+            in_=bias.rearrange("(o c) -> o c", o=1),
+        )
+    spread = psum.tile([P, C_ALL], F32, tag="bank")
+    nc.tensor.matmul(out=spread[:], lhsT=ones[:], rhs=bias_rows[:], start=True, stop=True)
+    bias_all = consts.tile([P, C_ALL], F32)
+    nc.vector.tensor_copy(out=bias_all[:], in_=spread[:])
+    return bias_all
+
+
+def load_chunk(nc, x_pool, x_rows, b, h):
+    raws = []
+    for g in range(PASSES):
+        raw = x_pool.tile([P, PACK, CHUNK], BF16)
+        nc.sync.dma_start(
+            out=raw[:],
+            in_=x_rows[b, g * K_PASS : (g + 1) * K_PASS, h * CHUNK : (h + 1) * CHUNK].rearrange(
+                "(p t) w -> p t w", t=PACK
+            ),
+        )
+        raws.append(raw)
+    return raws
+
+
+def regroup(nc, grouped_pool, raw):
+    grouped = grouped_pool.tile([P, CHUNK * PACK], BF16, align_bytes=64)
+    src = raw[:].rearrange(
+        "p t (pair half quad m) -> p half m pair quad t", half=HALVES, quad=QUADS, m=QUAD
+    )
+    dst = grouped[:].rearrange(
+        "p (half m pair quad t) -> p half m pair quad t", half=HALVES, m=QUAD, quad=QUADS, t=PACK
+    )
+    for half in range(HALVES):
+        nc.vector.tensor_copy(out=dst[:, half, :, :V_PAIRS], in_=src[:, half, :, :V_PAIRS])
+        nc.scalar.copy(out=dst[:, half, :, V_PAIRS:], in_=src[:, half, :, V_PAIRS:])
+    return grouped
+
+
+def quantise(nc, codes_pool, grouped):
+    codes = codes_pool.tile([P, CHUNK], U32, align_bytes=64)
+    scales = codes_pool.tile([P, CHUNK], U8, align_bytes=64)
+    nc.vector.quantize_mx(out=codes[:].bitcast(FP8X4), scales=scales[:], in_=grouped[:])
+    return codes, scales
+
+
+def multiply(nc, psum, quantised, w_words, w_planes, half, m):
+    cols = slice((half * QUAD + m) * P, (half * QUAD + m + 1) * P)
+    bank = psum.tile([P, C_ALL], F32, tag="bank")
+    for g in range(PASSES):
+        codes, scales = quantised[g]
+        nc.tensor.matmul_mx(
+            out=bank[:],
+            lhsT=codes[:, cols].bitcast(FP8X4),
+            lhsT_scale=scales[:, cols],
+            rhs=w_words[:, g, :].bitcast(FP8X4),
+            rhs_scale=w_planes[:, g, :],
+            start=(g == 0),
+            stop=(g == PASSES - 1),
+        )
+    return bank
+
+
+def tile_selfattention3d_pb_t_kernel(
+    tc,
+    x,
+    w_theta_words,
+    w_theta_scales,
+    b_theta,
+    w_phi_words,
+    w_phi_scales,
+    b_phi,
+    w_g_words,
+    w_g_scales,
+    b_g,
+    out_0,
+    out_1,
+    out_2,
+):
+    nc = tc.nc
+    x_rows = x.rearrange("b c f i j -> b c (f i j)")
+
+    with ExitStack() as ctx:
+        consts = ctx.enter_context(tc.tile_pool(name="consts", bufs=1))
+        x_pool = ctx.enter_context(tc.tile_pool(name="x", bufs=8))
+        grouped_pool = ctx.enter_context(tc.tile_pool(name="grouped", bufs=4))
+        codes_pool = ctx.enter_context(tc.tile_pool(name="codes", bufs=4))
+        work = ctx.enter_context(tc.tile_pool(name="work", bufs=3))
+        results = ctx.enter_context(tc.tile_pool(name="results", bufs=3))
+        psum = ctx.enter_context(tc.psum_pool(name="psum", bufs=8))
+
+        chunks = [(b, h) for b in range(BATCH) for h in range(CHUNKS)]
+
+        loaded = {chunks[0]: load_chunk(nc, x_pool, x_rows, chunks[0][0], chunks[0][1])}
+        w_words, w_planes = load_weights(
+            nc,
+            consts,
+            [
+                (w_theta_words, w_theta_scales, 0, C_THETA),
+                (w_phi_words, w_phi_scales, C_THETA, C_PHI),
+                (w_g_words, w_g_scales, C_THETA + C_PHI, C_G),
+            ],
+        )
+        bias_all = spread_biases(
+            nc,
+            consts,
+            psum,
+            [(b_theta, 0, C_THETA), (b_phi, C_THETA, C_PHI), (b_g, C_THETA + C_PHI, C_G)],
+        )
+
+        for b, h in chunks:
+            if (b, h) not in loaded:
+                loaded[(b, h)] = load_chunk(nc, x_pool, x_rows, b, h)
+            quantised = [quantise(nc, codes_pool, regroup(nc, grouped_pool, raw)) for raw in loaded[(b, h)]]
+
+            theta = results.tile([P, HALVES, QUAD, C_THETA], F32)
+            phi = results.tile([P, WINDOWS, C_PHI], F32)
+            pooled_biased = results.tile([P, WINDOWS, C_POOLED], F32)
+
+            for window in range(WINDOWS):
+                members = [(half, side) for half in range(HALVES) for side in range(SIDES)]
+                banks = [
+                    multiply(nc, psum, quantised, w_words, w_planes, half, SIDES * window + side)
+                    for half, side in members
+                ]
+
+                pooled = work.tile([P, C_POOLED], F32)
+                theta_sum = work.tile([P, HALVES, SIDES, C_THETA], F32)
+                nc.scalar.copy(out=pooled[:], in_=banks[0][:, C_THETA:])
+                for (half, side), bank in list(zip(members, banks))[1:]:
+                    nc.vector.tensor_tensor(out=pooled[:], in0=bank[:, C_THETA:], in1=pooled[:], op=MAX)
+                    nc.vector.tensor_tensor(
+                        out=theta_sum[:, half, side, :], in0=bank[:, :C_THETA], in1=bias_all[:, :C_THETA], op=ADD
+                    )
+                nc.vector.tensor_tensor(
+                    out=pooled_biased[:, window, :], in0=pooled[:], in1=bias_all[:, C_THETA:], op=ADD
+                )
+                nc.vector.tensor_tensor(
+                    out=theta_sum[:, 0, 0, :], in0=banks[0][:, :C_THETA], in1=bias_all[:, :C_THETA], op=ADD
+                )
+
+                nc.scalar.activation(
+                    out=theta[:, :, SIDES * window : SIDES * (window + 1), :], in_=theta_sum[:], func=TANH
+                )
+                nc.scalar.activation(out=phi[:, window, :], in_=pooled_biased[:, window, :C_PHI], func=TANH)
+
+            theta_rows = out_0[b, h * CHUNK : (h + 1) * CHUNK, :].rearrange(
+                "(pair half quad m) c -> half pair quad (m c)", half=HALVES, quad=QUADS, m=QUAD
+            )
+            for half in range(HALVES):
+                nc.sync.dma_start(out=theta_rows[half], in_=theta[:, half].rearrange("p m c -> p (m c)"))
+            pooled_rows = slice(h * POOLED_CHUNK, (h + 1) * POOLED_CHUNK)
+            nc.sync.dma_start(
+                out=out_1[b, pooled_rows, :].rearrange("(site window) c -> site (window c)", window=WINDOWS),
+                in_=phi[:].rearrange("p window c -> p (window c)"),
+            )
+            nc.sync.dma_start(
+                out=out_2[b, pooled_rows, :].rearrange("(site window) c -> site window c", window=WINDOWS),
+                in_=pooled_biased[:, :, C_PHI:],
+            )

@@ -97,14 +97,14 @@ def load_chunk(nc, x_pool, x_rows, b, h):
 def regroup(nc, grouped_pool, raw):
     grouped = grouped_pool.tile([P, CHUNK * PACK], BF16, align_bytes=64)
     src = raw[:].rearrange(
-        "p t (pair half quad m) -> p half m pair quad t", half=HALVES, quad=QUADS, m=QUAD
+        "p t (pair half quad m) -> p half pair quad t m", half=HALVES, quad=QUADS, m=QUAD
     )
     dst = grouped[:].rearrange(
-        "p (half m pair quad t) -> p half m pair quad t", half=HALVES, m=QUAD, quad=QUADS, t=PACK
+        "p (half m pair quad t) -> p half pair quad t m", half=HALVES, m=QUAD, quad=QUADS, t=PACK
     )
     for half in range(HALVES):
-        nc.vector.tensor_copy(out=dst[:, half, :, :V_PAIRS], in_=src[:, half, :, :V_PAIRS])
-        nc.scalar.copy(out=dst[:, half, :, V_PAIRS:], in_=src[:, half, :, V_PAIRS:])
+        nc.vector.tensor_copy(out=dst[:, half, :V_PAIRS], in_=src[:, half, :V_PAIRS])
+        nc.scalar.copy(out=dst[:, half, V_PAIRS:], in_=src[:, half, V_PAIRS:])
     return grouped
 
 

@@ -39,6 +39,10 @@ POOLED_CHUNK = CHUNK // 4
 
 V_PAIRS = 12
 
+MEMBERS = [(half, side) for half in range(HALVES) for side in range(SIDES)]
+
+CHUNKS_AHEAD = 4
+
 FLOPS = 2 * BATCH * LOCATIONS * CHANNELS * C_ALL
 
 assert PAIRS * QUADS == P
@@ -115,21 +119,63 @@ def quantise(nc, codes_pool, grouped):
     return codes, scales
 
 
-def multiply(nc, psum, quantised, w_words, w_planes, half, m):
-    cols = slice((half * QUAD + m) * P, (half * QUAD + m + 1) * P)
-    bank = psum.tile([P, C_ALL], F32, tag="bank")
-    for g in range(PASSES):
-        codes, scales = quantised[g]
-        nc.tensor.matmul_mx(
-            out=bank[:],
-            lhsT=codes[:, cols].bitcast(FP8X4),
-            lhsT_scale=scales[:, cols],
-            rhs=w_words[:, g, :].bitcast(FP8X4),
-            rhs_scale=w_planes[:, g, :],
-            start=(g == 0),
-            stop=(g == PASSES - 1),
+def multiply_window(nc, psum, quantised, w_words, w_planes, window):
+    banks = []
+    for half, side in MEMBERS:
+        first = (half * QUAD + SIDES * window + side) * P
+        bank = psum.tile([P, C_ALL], F32, tag="bank")
+        for g in range(PASSES):
+            codes, scales = quantised[g]
+            nc.tensor.matmul_mx(
+                out=bank[:],
+                lhsT=codes[:, first : first + P].bitcast(FP8X4),
+                lhsT_scale=scales[:, first : first + P],
+                rhs=w_words[:, g, :].bitcast(FP8X4),
+                rhs_scale=w_planes[:, g, :],
+                start=(g == 0),
+                stop=(g == PASSES - 1),
+            )
+        banks.append(bank)
+    return banks
+
+
+def lift_first_member(nc, work, banks):
+    pooled = work.tile([P, C_POOLED], F32)
+    nc.scalar.copy(out=pooled[:], in_=banks[0][:, C_THETA:])
+    return pooled
+
+
+def fold_members(nc, banks, pooled, bias_all, theta, pooled_biased, window):
+    for (half, side), bank in list(zip(MEMBERS, banks))[1:]:
+        nc.vector.tensor_tensor(out=pooled[:], in0=bank[:, C_THETA:], in1=pooled[:], op=MAX)
+        nc.vector.tensor_tensor(
+            out=theta[:, half, SIDES * window + side, :], in0=bank[:, :C_THETA], in1=bias_all[:, :C_THETA], op=ADD
         )
-    return bank
+    nc.vector.tensor_tensor(out=pooled_biased[:, window, :], in0=pooled[:], in1=bias_all[:, C_THETA:], op=ADD)
+    nc.vector.tensor_tensor(
+        out=theta[:, 0, SIDES * window, :], in0=banks[0][:, :C_THETA], in1=bias_all[:, :C_THETA], op=ADD
+    )
+
+
+def finish_chunk(nc, results, theta, pooled_biased, out_0, out_1, out_2, b, h):
+    phi = results.tile([P, WINDOWS, C_PHI], F32)
+    nc.scalar.activation(out=theta[:], in_=theta[:], func=TANH)
+    nc.scalar.activation(out=phi[:], in_=pooled_biased[:, :, :C_PHI], func=TANH)
+
+    theta_rows = out_0[b, h * CHUNK : (h + 1) * CHUNK, :].rearrange(
+        "(pair half quad m) c -> half pair quad (m c)", half=HALVES, quad=QUADS, m=QUAD
+    )
+    for half in range(HALVES):
+        nc.sync.dma_start(out=theta_rows[half], in_=theta[:, half].rearrange("p m c -> p (m c)"))
+    pooled_rows = slice(h * POOLED_CHUNK, (h + 1) * POOLED_CHUNK)
+    nc.sync.dma_start(
+        out=out_1[b, pooled_rows, :].rearrange("(site window) c -> site (window c)", window=WINDOWS),
+        in_=phi[:].rearrange("p window c -> p (window c)"),
+    )
+    nc.sync.dma_start(
+        out=out_2[b, pooled_rows, :].rearrange("(site window) c -> site window c", window=WINDOWS),
+        in_=pooled_biased[:, :, C_PHI:],
+    )
 
 
 def tile_selfattention3d_pb_t_kernel(
@@ -150,19 +196,27 @@ def tile_selfattention3d_pb_t_kernel(
 ):
     nc = tc.nc
     x_rows = x.rearrange("b c f i j -> b c (f i j)")
+    chunks = [(b, h) for b in range(BATCH) for h in range(CHUNKS)]
+    n_chunks = len(chunks)
 
     with ExitStack() as ctx:
         consts = ctx.enter_context(tc.tile_pool(name="consts", bufs=1))
-        x_pool = ctx.enter_context(tc.tile_pool(name="x", bufs=8))
-        grouped_pool = ctx.enter_context(tc.tile_pool(name="grouped", bufs=4))
-        codes_pool = ctx.enter_context(tc.tile_pool(name="codes", bufs=4))
+        x_pool = ctx.enter_context(tc.tile_pool(name="x", bufs=PASSES * CHUNKS_AHEAD))
+        grouped_pool = ctx.enter_context(tc.tile_pool(name="grouped", bufs=PASSES * 2))
+        codes_pool = ctx.enter_context(tc.tile_pool(name="codes", bufs=PASSES * 2))
         work = ctx.enter_context(tc.tile_pool(name="work", bufs=3))
         results = ctx.enter_context(tc.tile_pool(name="results", bufs=3))
-        psum = ctx.enter_context(tc.psum_pool(name="psum", bufs=8))
+        psum = ctx.enter_context(tc.psum_pool(name="psum", bufs=2 * len(MEMBERS)))
+        ctx.enter_context(tc.manual_schedule())
 
-        chunks = [(b, h) for b in range(BATCH) for h in range(CHUNKS)]
+        raws = {}
+        grouped = {}
+        banks = {}
+        pooled = {}
+        theta = {}
+        pooled_biased = {}
 
-        loaded = {chunks[0]: load_chunk(nc, x_pool, x_rows, chunks[0][0], chunks[0][1])}
+        raws[0] = load_chunk(nc, x_pool, x_rows, chunks[0][0], chunks[0][1])
         w_words, w_planes = load_weights(
             nc,
             consts,
@@ -178,54 +232,42 @@ def tile_selfattention3d_pb_t_kernel(
             psum,
             [(b_theta, 0, C_THETA), (b_phi, C_THETA, C_PHI), (b_g, C_THETA + C_PHI, C_G)],
         )
+        for i in range(1, CHUNKS_AHEAD):
+            raws[i] = load_chunk(nc, x_pool, x_rows, chunks[i][0], chunks[i][1])
+        grouped[0] = [regroup(nc, grouped_pool, raw) for raw in raws[0]]
 
-        for b, h in chunks:
-            if (b, h) not in loaded:
-                loaded[(b, h)] = load_chunk(nc, x_pool, x_rows, b, h)
-            quantised = [quantise(nc, codes_pool, regroup(nc, grouped_pool, raw)) for raw in loaded[(b, h)]]
+        for i in range(n_chunks):
+            before = i - 1
+            after = i + 1
+            if i + CHUNKS_AHEAD < n_chunks:
+                ahead = i + CHUNKS_AHEAD
+                raws[ahead] = load_chunk(nc, x_pool, x_rows, chunks[ahead][0], chunks[ahead][1])
 
-            theta = results.tile([P, HALVES, QUAD, C_THETA], F32)
-            phi = results.tile([P, WINDOWS, C_PHI], F32)
-            pooled_biased = results.tile([P, WINDOWS, C_POOLED], F32)
+            quantised = [quantise(nc, codes_pool, tile_g) for tile_g in grouped[i]]
+            theta[i] = results.tile([P, HALVES, QUAD, C_THETA], F32, name="theta", tag="theta")
+            pooled_biased[i] = results.tile([P, WINDOWS, C_POOLED], F32, name="pooled_biased", tag="pooled_biased")
+            banks[0] = multiply_window(nc, psum, quantised, w_words, w_planes, 0)
 
-            for window in range(WINDOWS):
-                members = [(half, side) for half in range(HALVES) for side in range(SIDES)]
-                banks = [
-                    multiply(nc, psum, quantised, w_words, w_planes, half, SIDES * window + side)
-                    for half, side in members
-                ]
+            if before >= 0:
+                pooled[1] = lift_first_member(nc, work, banks[1])
+                fold_members(nc, banks[1], pooled[1], bias_all, theta[before], pooled_biased[before], 1)
+            banks[1] = multiply_window(nc, psum, quantised, w_words, w_planes, 1)
 
-                pooled = work.tile([P, C_POOLED], F32)
-                theta_sum = work.tile([P, HALVES, SIDES, C_THETA], F32)
-                nc.scalar.copy(out=pooled[:], in_=banks[0][:, C_THETA:])
-                for (half, side), bank in list(zip(members, banks))[1:]:
-                    nc.vector.tensor_tensor(out=pooled[:], in0=bank[:, C_THETA:], in1=pooled[:], op=MAX)
-                    nc.vector.tensor_tensor(
-                        out=theta_sum[:, half, side, :], in0=bank[:, :C_THETA], in1=bias_all[:, :C_THETA], op=ADD
-                    )
-                nc.vector.tensor_tensor(
-                    out=pooled_biased[:, window, :], in0=pooled[:], in1=bias_all[:, C_THETA:], op=ADD
+            if after < n_chunks:
+                grouped[after] = [regroup(nc, grouped_pool, raws[after][0])]
+            pooled[0] = lift_first_member(nc, work, banks[0])
+            if before >= 0:
+                finish_chunk(
+                    nc, results, theta[before], pooled_biased[before], out_0, out_1, out_2,
+                    chunks[before][0], chunks[before][1],
                 )
-                nc.vector.tensor_tensor(
-                    out=theta_sum[:, 0, 0, :], in0=banks[0][:, :C_THETA], in1=bias_all[:, :C_THETA], op=ADD
-                )
+            if after < n_chunks:
+                grouped[after].append(regroup(nc, grouped_pool, raws[after][1]))
+            fold_members(nc, banks[0], pooled[0], bias_all, theta[i], pooled_biased[i], 0)
 
-                nc.scalar.activation(
-                    out=theta[:, :, SIDES * window : SIDES * (window + 1), :], in_=theta_sum[:], func=TANH
-                )
-                nc.scalar.activation(out=phi[:, window, :], in_=pooled_biased[:, window, :C_PHI], func=TANH)
-
-            theta_rows = out_0[b, h * CHUNK : (h + 1) * CHUNK, :].rearrange(
-                "(pair half quad m) c -> half pair quad (m c)", half=HALVES, quad=QUADS, m=QUAD
-            )
-            for half in range(HALVES):
-                nc.sync.dma_start(out=theta_rows[half], in_=theta[:, half].rearrange("p m c -> p (m c)"))
-            pooled_rows = slice(h * POOLED_CHUNK, (h + 1) * POOLED_CHUNK)
-            nc.sync.dma_start(
-                out=out_1[b, pooled_rows, :].rearrange("(site window) c -> site (window c)", window=WINDOWS),
-                in_=phi[:].rearrange("p window c -> p (window c)"),
-            )
-            nc.sync.dma_start(
-                out=out_2[b, pooled_rows, :].rearrange("(site window) c -> site window c", window=WINDOWS),
-                in_=pooled_biased[:, :, C_PHI:],
-            )
+        last = n_chunks - 1
+        pooled[1] = lift_first_member(nc, work, banks[1])
+        fold_members(nc, banks[1], pooled[1], bias_all, theta[last], pooled_biased[last], 1)
+        finish_chunk(
+            nc, results, theta[last], pooled_biased[last], out_0, out_1, out_2, chunks[last][0], chunks[last][1]
+        )

@@ -1,6 +1,7 @@
 from contextlib import ExitStack
 
 import concourse.mybir as mybir
+from concourse.masks import make_identity
 
 BF16 = mybir.dt.bfloat16
 F32 = mybir.dt.float32
@@ -8,9 +9,9 @@ I32 = mybir.dt.int32
 U32 = mybir.dt.uint32
 U8 = mybir.dt.uint8
 FP8X4 = mybir.dt.float8_e4m3fn_x4
-ADD = mybir.AluOpType.add
 MAX = mybir.AluOpType.max
 TANH = mybir.ActivationFunctionType.Tanh
+IDENTITY = mybir.ActivationFunctionType.Identity
 
 P = 128
 PACK = 4
@@ -20,33 +21,24 @@ BATCH = 2
 CHANNELS = 1024
 PASSES = CHANNELS // K_PASS
 LOCATIONS = 16 * 16 * 16
+SIDE = 16
 
-C_THETA = 128
-C_PHI = 128
-C_G = 256
-C_POOLED = C_PHI + C_G
-C_ALL = C_THETA + C_POOLED
+C_ALL = 512
+THETA = 0
+POOLED_TILES = (1, 2, 3)
 
-PAIRS = 32
-HALVES = 2
-QUADS = 4
-QUAD = 4
-WINDOWS = 2
-SIDES = 2
-CHUNK = PAIRS * HALVES * QUADS * QUAD
-CHUNKS = LOCATIONS // CHUNK
+BLOCK = 512
+POOLED_BLOCK = BLOCK // 4
+BLOCKS = 2
+CHUNK = BLOCKS * BLOCK
 POOLED_CHUNK = CHUNK // 4
+CHUNKS = LOCATIONS // CHUNK
+THETA_RUN = BLOCK // P
+POOLED_RUN = POOLED_CHUNK // P
 
-V_PAIRS = 12
-
-MEMBERS = [(half, side) for half in range(HALVES) for side in range(SIDES)]
-
-CHUNKS_AHEAD = 4
+V_LOCATIONS = 576
 
 FLOPS = 2 * BATCH * LOCATIONS * CHANNELS * C_ALL
-
-assert PAIRS * QUADS == P
-assert WINDOWS * SIDES == QUAD
 
 
 def load_weights(nc, consts, weights):
@@ -67,21 +59,19 @@ def load_weights(nc, consts, weights):
     return w_words, w_planes
 
 
-def spread_biases(nc, consts, psum, biases):
-    bias_rows = consts.tile([P, C_ALL], BF16)
-    ones = consts.tile([P, P], BF16)
-    nc.vector.memset(bias_rows[:], 0.0)
-    nc.vector.memset(ones[:], 1.0)
-    for bias, first, count in biases:
-        nc.scalar.dma_start(
-            out=bias_rows[0:1, first : first + count],
-            in_=bias.rearrange("(o c) -> o c", o=1),
-        )
-    spread = psum.tile([P, C_ALL], F32, tag="bank")
-    nc.tensor.matmul(out=spread[:], lhsT=ones[:], rhs=bias_rows[:], start=True, stop=True)
-    bias_all = consts.tile([P, C_ALL], F32)
-    nc.vector.tensor_copy(out=bias_all[:], in_=spread[:])
-    return bias_all
+def load_biases(nc, consts, psum_turned, identity, b_theta, b_phi, b_g):
+    rows_bf16 = consts.tile([P, P], BF16)
+    nc.vector.memset(rows_bf16[:], 0.0)
+    nc.scalar.dma_start(out=rows_bf16[0:1, :], in_=b_theta.rearrange("(k c) -> k c", k=1))
+    nc.scalar.dma_start(out=rows_bf16[1:2, :], in_=b_phi.rearrange("(k c) -> k c", k=1))
+    nc.scalar.dma_start(out=rows_bf16[2:4, :], in_=b_g.rearrange("(k c) -> k c", k=2))
+    rows = consts.tile([P, P], F32)
+    nc.vector.tensor_copy(out=rows[:], in_=rows_bf16[:])
+    columns = psum_turned.tile([P, P], F32, tag="theta_turned")
+    nc.tensor.transpose(columns[:], rows[:], identity[:])
+    biases = consts.tile([P, 4], F32)
+    nc.vector.tensor_copy(out=biases[:], in_=columns[:, 0:4])
+    return biases
 
 
 def load_chunk(nc, x_pool, x_rows, b, h):
@@ -99,83 +89,40 @@ def load_chunk(nc, x_pool, x_rows, b, h):
 
 
 def regroup(nc, grouped_pool, raw):
-    grouped = grouped_pool.tile([P, CHUNK * PACK], BF16, align_bytes=64)
-    src = raw[:].rearrange(
-        "p t (pair half quad m) -> p half pair quad t m", half=HALVES, quad=QUADS, m=QUAD
-    )
-    dst = grouped[:].rearrange(
-        "p (half m pair quad t) -> p half pair quad t m", half=HALVES, m=QUAD, quad=QUADS, t=PACK
-    )
-    for half in range(HALVES):
-        nc.vector.tensor_copy(out=dst[:, half, :V_PAIRS], in_=src[:, half, :V_PAIRS])
-        nc.scalar.copy(out=dst[:, half, V_PAIRS:], in_=src[:, half, V_PAIRS:])
+    grouped = grouped_pool.tile([P, CHUNK, PACK], BF16, align_bytes=64)
+    src = raw[:].rearrange("p t (c i) -> p c t i", i=4)
+    dst = grouped[:].rearrange("p (c i) t -> p c t i", i=4)
+    split = V_LOCATIONS // 4
+    nc.vector.tensor_copy(out=dst[:, :split], in_=src[:, :split])
+    nc.scalar.copy(out=dst[:, split:], in_=src[:, split:])
     return grouped
 
 
 def quantise(nc, codes_pool, grouped):
     codes = codes_pool.tile([P, CHUNK], U32, align_bytes=64)
     scales = codes_pool.tile([P, CHUNK], U8, align_bytes=64)
-    nc.vector.quantize_mx(out=codes[:].bitcast(FP8X4), scales=scales[:], in_=grouped[:])
+    nc.vector.quantize_mx(
+        out=codes[:].bitcast(FP8X4), scales=scales[:], in_=grouped[:].rearrange("p w t -> p (w t)")
+    )
     return codes, scales
 
 
-def multiply_window(nc, psum, quantised, w_words, w_planes, window):
-    banks = []
-    for half, side in MEMBERS:
-        first = (half * QUAD + SIDES * window + side) * P
-        bank = psum.tile([P, C_ALL], F32, tag="bank")
-        for g in range(PASSES):
-            codes, scales = quantised[g]
-            nc.tensor.matmul_mx(
-                out=bank[:],
-                lhsT=codes[:, first : first + P].bitcast(FP8X4),
-                lhsT_scale=scales[:, first : first + P],
-                rhs=w_words[:, g, :].bitcast(FP8X4),
-                rhs_scale=w_planes[:, g, :],
-                start=(g == 0),
-                stop=(g == PASSES - 1),
-            )
-        banks.append(bank)
-    return banks
-
-
-def lift_first_member(nc, work, banks):
-    pooled = work.tile([P, C_POOLED], F32)
-    nc.scalar.copy(out=pooled[:], in_=banks[0][:, C_THETA:])
-    return pooled
-
-
-def fold_members(nc, banks, pooled, bias_all, theta, pooled_biased, window):
-    for (half, side), bank in list(zip(MEMBERS, banks))[1:]:
-        nc.vector.tensor_tensor(out=pooled[:], in0=bank[:, C_THETA:], in1=pooled[:], op=MAX)
-        nc.vector.tensor_tensor(
-            out=theta[:, half, SIDES * window + side, :], in0=bank[:, :C_THETA], in1=bias_all[:, :C_THETA], op=ADD
+def multiply(nc, psum_sums, quantised, w_words, w_planes, channel_tile, block):
+    w_cols = slice(channel_tile * P, (channel_tile + 1) * P)
+    x_cols = slice(block * BLOCK, (block + 1) * BLOCK)
+    sums = psum_sums.tile([P, BLOCK], F32)
+    for g in range(PASSES):
+        codes, scales = quantised[g]
+        nc.tensor.matmul_mx(
+            out=sums[:],
+            lhsT=w_words[:, g, w_cols].bitcast(FP8X4),
+            lhsT_scale=w_planes[:, g, w_cols],
+            rhs=codes[:, x_cols].bitcast(FP8X4),
+            rhs_scale=scales[:, x_cols],
+            start=(g == 0),
+            stop=(g == PASSES - 1),
         )
-    nc.vector.tensor_tensor(out=pooled_biased[:, window, :], in0=pooled[:], in1=bias_all[:, C_THETA:], op=ADD)
-    nc.vector.tensor_tensor(
-        out=theta[:, 0, SIDES * window, :], in0=banks[0][:, :C_THETA], in1=bias_all[:, :C_THETA], op=ADD
-    )
-
-
-def finish_chunk(nc, results, theta, pooled_biased, out_0, out_1, out_2, b, h):
-    phi = results.tile([P, WINDOWS, C_PHI], F32)
-    nc.scalar.activation(out=theta[:], in_=theta[:], func=TANH)
-    nc.scalar.activation(out=phi[:], in_=pooled_biased[:, :, :C_PHI], func=TANH)
-
-    theta_rows = out_0[b, h * CHUNK : (h + 1) * CHUNK, :].rearrange(
-        "(pair half quad m) c -> half pair quad (m c)", half=HALVES, quad=QUADS, m=QUAD
-    )
-    for half in range(HALVES):
-        nc.sync.dma_start(out=theta_rows[half], in_=theta[:, half].rearrange("p m c -> p (m c)"))
-    pooled_rows = slice(h * POOLED_CHUNK, (h + 1) * POOLED_CHUNK)
-    nc.sync.dma_start(
-        out=out_1[b, pooled_rows, :].rearrange("(site window) c -> site (window c)", window=WINDOWS),
-        in_=phi[:].rearrange("p window c -> p (window c)"),
-    )
-    nc.sync.dma_start(
-        out=out_2[b, pooled_rows, :].rearrange("(site window) c -> site window c", window=WINDOWS),
-        in_=pooled_biased[:, :, C_PHI:],
-    )
+    return sums
 
 
 def tile_selfattention3d_pb_t_kernel(
@@ -196,78 +143,94 @@ def tile_selfattention3d_pb_t_kernel(
 ):
     nc = tc.nc
     x_rows = x.rearrange("b c f i j -> b c (f i j)")
-    chunks = [(b, h) for b in range(BATCH) for h in range(CHUNKS)]
-    n_chunks = len(chunks)
 
     with ExitStack() as ctx:
         consts = ctx.enter_context(tc.tile_pool(name="consts", bufs=1))
-        x_pool = ctx.enter_context(tc.tile_pool(name="x", bufs=PASSES * CHUNKS_AHEAD))
-        grouped_pool = ctx.enter_context(tc.tile_pool(name="grouped", bufs=PASSES * 2))
-        codes_pool = ctx.enter_context(tc.tile_pool(name="codes", bufs=PASSES * 2))
+        x_pool = ctx.enter_context(tc.tile_pool(name="x", bufs=8))
+        grouped_pool = ctx.enter_context(tc.tile_pool(name="grouped", bufs=4))
+        codes_pool = ctx.enter_context(tc.tile_pool(name="codes", bufs=4))
         work = ctx.enter_context(tc.tile_pool(name="work", bufs=3))
         results = ctx.enter_context(tc.tile_pool(name="results", bufs=3))
-        psum = ctx.enter_context(tc.psum_pool(name="psum", bufs=2 * len(MEMBERS)))
-        ctx.enter_context(tc.manual_schedule())
+        psum_sums = ctx.enter_context(tc.psum_pool(name="psum_sums", bufs=5))
+        psum_turned = ctx.enter_context(tc.psum_pool(name="psum_turned", bufs=1))
 
-        raws = {}
-        grouped = {}
-        banks = {}
-        pooled = {}
-        theta = {}
-        pooled_biased = {}
+        chunks = [(b, h) for b in range(BATCH) for h in range(CHUNKS)]
 
-        raws[0] = load_chunk(nc, x_pool, x_rows, chunks[0][0], chunks[0][1])
+        first_raws = load_chunk(nc, x_pool, x_rows, chunks[0][0], chunks[0][1])
         w_words, w_planes = load_weights(
             nc,
             consts,
-            [
-                (w_theta_words, w_theta_scales, 0, C_THETA),
-                (w_phi_words, w_phi_scales, C_THETA, C_PHI),
-                (w_g_words, w_g_scales, C_THETA + C_PHI, C_G),
-            ],
+            [(w_theta_words, w_theta_scales, 0, 128), (w_phi_words, w_phi_scales, 128, 128), (w_g_words, w_g_scales, 256, 256)],
         )
-        bias_all = spread_biases(
-            nc,
-            consts,
-            psum,
-            [(b_theta, 0, C_THETA), (b_phi, C_THETA, C_PHI), (b_g, C_THETA + C_PHI, C_G)],
-        )
-        for i in range(1, CHUNKS_AHEAD):
-            raws[i] = load_chunk(nc, x_pool, x_rows, chunks[i][0], chunks[i][1])
-        grouped[0] = [regroup(nc, grouped_pool, raw) for raw in raws[0]]
+        identity = consts.tile([P, P], F32)
+        make_identity(nc, identity[:])
+        biases = load_biases(nc, consts, psum_turned, identity, b_theta, b_phi, b_g)
 
-        for i in range(n_chunks):
-            before = i - 1
-            after = i + 1
-            if i + CHUNKS_AHEAD < n_chunks:
-                ahead = i + CHUNKS_AHEAD
-                raws[ahead] = load_chunk(nc, x_pool, x_rows, chunks[ahead][0], chunks[ahead][1])
+        grouped = [regroup(nc, grouped_pool, raw) for raw in first_raws]
+        for i, (b, h) in enumerate(chunks):
+            quantised = [quantise(nc, codes_pool, grouped_g) for grouped_g in grouped]
+            if i + 1 < len(chunks):
+                raws = load_chunk(nc, x_pool, x_rows, chunks[i + 1][0], chunks[i + 1][1])
+                grouped = [regroup(nc, grouped_pool, raw) for raw in raws]
 
-            quantised = [quantise(nc, codes_pool, tile_g) for tile_g in grouped[i]]
-            theta[i] = results.tile([P, HALVES, QUAD, C_THETA], F32, name="theta", tag="theta")
-            pooled_biased[i] = results.tile([P, WINDOWS, C_POOLED], F32, name="pooled_biased", tag="pooled_biased")
-            banks[0] = multiply_window(nc, psum, quantised, w_words, w_planes, 0)
+            pooled = work.tile([P, len(POOLED_TILES), POOLED_CHUNK], F32)
+            for block in range(BLOCKS):
+                for k, channel_tile in enumerate(POOLED_TILES):
+                    sums = multiply(nc, psum_sums, quantised, w_words, w_planes, channel_tile, block)
+                    nc.vector.tensor_reduce(
+                        out=pooled[:, k, block * POOLED_BLOCK : (block + 1) * POOLED_BLOCK].rearrange(
+                            "c (pair j) -> c pair j", j=SIDE // 2
+                        ),
+                        in_=sums[:].rearrange(
+                            "c (pair half j side) -> c pair j half side", half=2, j=SIDE // 2, side=2
+                        ),
+                        axis=mybir.AxisListType.XY,
+                        op=MAX,
+                    )
 
-            if before >= 0:
-                pooled[1] = lift_first_member(nc, work, banks[1])
-                fold_members(nc, banks[1], pooled[1], bias_all, theta[before], pooled_biased[before], 1)
-            banks[1] = multiply_window(nc, psum, quantised, w_words, w_planes, 1)
-
-            if after < n_chunks:
-                grouped[after] = [regroup(nc, grouped_pool, raws[after][0])]
-            pooled[0] = lift_first_member(nc, work, banks[0])
-            if before >= 0:
-                finish_chunk(
-                    nc, results, theta[before], pooled_biased[before], out_0, out_1, out_2,
-                    chunks[before][0], chunks[before][1],
+                sums = multiply(nc, psum_sums, quantised, w_words, w_planes, THETA, block)
+                theta_by_channel = work.tile([P, THETA_RUN, P], F32)
+                nc.scalar.activation(
+                    out=theta_by_channel[:],
+                    in_=sums[:].rearrange("c (p t) -> c t p", t=THETA_RUN),
+                    func=TANH,
+                    bias=biases[:, THETA : THETA + 1],
                 )
-            if after < n_chunks:
-                grouped[after].append(regroup(nc, grouped_pool, raws[after][1]))
-            fold_members(nc, banks[0], pooled[0], bias_all, theta[i], pooled_biased[i], 0)
+                theta_turned = psum_turned.tile([P, THETA_RUN, P], F32)
+                for t in range(THETA_RUN):
+                    nc.tensor.transpose(theta_turned[:, t, :], theta_by_channel[:, t, :], identity[:])
+                theta = results.tile([P, THETA_RUN, P], F32)
+                nc.scalar.copy(out=theta[:], in_=theta_turned[:])
+                first = h * CHUNK + block * BLOCK
+                nc.sync.dma_start(
+                    out=out_0[b, first : first + BLOCK, :].rearrange("(p t) c -> p (t c)", t=THETA_RUN),
+                    in_=theta[:].rearrange("p t c -> p (t c)"),
+                )
 
-        last = n_chunks - 1
-        pooled[1] = lift_first_member(nc, work, banks[1])
-        fold_members(nc, banks[1], pooled[1], bias_all, theta[last], pooled_biased[last], 1)
-        finish_chunk(
-            nc, results, theta[last], pooled_biased[last], out_0, out_1, out_2, chunks[last][0], chunks[last][1]
-        )
+            pooled_by_channel = work.tile([P, len(POOLED_TILES), POOLED_RUN, P], F32)
+            for k, channel_tile in enumerate(POOLED_TILES):
+                nc.scalar.activation(
+                    out=pooled_by_channel[:, k],
+                    in_=pooled[:, k, :].rearrange("c (p t) -> c t p", t=POOLED_RUN),
+                    func=(TANH if k == 0 else IDENTITY),
+                    bias=biases[:, channel_tile : channel_tile + 1],
+                )
+            phi_turned = psum_turned.tile([P, POOLED_RUN, P], F32)
+            g_turned = psum_turned.tile([P, POOLED_RUN, 2, P], F32)
+            for t in range(POOLED_RUN):
+                nc.tensor.transpose(phi_turned[:, t, :], pooled_by_channel[:, 0, t, :], identity[:])
+                for half_of_g in range(2):
+                    nc.tensor.transpose(
+                        g_turned[:, t, half_of_g, :], pooled_by_channel[:, 1 + half_of_g, t, :], identity[:]
+                    )
+            phi = results.tile([P, POOLED_RUN * P], F32)
+            g_out = results.tile([P, POOLED_RUN * 2 * P], F32)
+            nc.scalar.copy(out=phi[:], in_=phi_turned[:].rearrange("p t c -> p (t c)"))
+            nc.scalar.copy(out=g_out[:], in_=g_turned[:].rearrange("p t k c -> p (t k c)"))
+            pooled_rows = slice(h * POOLED_CHUNK, (h + 1) * POOLED_CHUNK)
+            nc.sync.dma_start(
+                out=out_1[b, pooled_rows, :].rearrange("(p t) c -> p (t c)", t=POOLED_RUN), in_=phi[:]
+            )
+            nc.sync.dma_start(
+                out=out_2[b, pooled_rows, :].rearrange("(p t) c -> p (t c)", t=POOLED_RUN), in_=g_out[:]
+            )

@@ -10,6 +10,8 @@ U32 = mybir.dt.uint32
 U8 = mybir.dt.uint8
 FP8X4 = mybir.dt.float8_e4m3fn_x4
 MAX = mybir.AluOpType.max
+MULT = mybir.AluOpType.mult
+ADD = mybir.AluOpType.add
 TANH = mybir.ActivationFunctionType.Tanh
 IDENTITY = mybir.ActivationFunctionType.Identity
 
@@ -36,7 +38,8 @@ CHUNKS = LOCATIONS // CHUNK
 THETA_RUN = BLOCK // P
 POOLED_RUN = POOLED_CHUNK // P
 
-V_LOCATIONS = 576
+V_LOCATIONS = 368
+G_LOCATIONS = 256
 
 FLOPS = 2 * BATCH * LOCATIONS * CHANNELS * C_ALL
 
@@ -93,8 +96,17 @@ def regroup(nc, grouped_pool, raw):
     src = raw[:].rearrange("p t (c i) -> p c t i", i=4)
     dst = grouped[:].rearrange("p (c i) t -> p c t i", i=4)
     split = V_LOCATIONS // 4
+    last = (CHUNK - G_LOCATIONS) // 4
     nc.vector.tensor_copy(out=dst[:, :split], in_=src[:, :split])
-    nc.scalar.copy(out=dst[:, split:], in_=src[:, split:])
+    nc.scalar.copy(out=dst[:, split:last], in_=src[:, split:last])
+    nc.gpsimd.tensor_scalar(
+        out=grouped[:, CHUNK - G_LOCATIONS :, :],
+        in0=raw[:, :, CHUNK - G_LOCATIONS :].rearrange("p t w -> p w t"),
+        scalar1=1.0,
+        scalar2=0.0,
+        op0=MULT,
+        op1=ADD,
+    )
     return grouped
 
 

@@ -110,13 +110,21 @@ def regroup(nc, grouped_pool, raw):
     return grouped
 
 
-def quantise(nc, codes_pool, grouped):
-    codes = codes_pool.tile([P, CHUNK], U32, align_bytes=64)
-    scales = codes_pool.tile([P, CHUNK], U8, align_bytes=64)
-    nc.vector.quantize_mx(
-        out=codes[:].bitcast(FP8X4), scales=scales[:], in_=grouped[:].rearrange("p w t -> p (w t)")
-    )
-    return codes, scales
+def quantise(nc, codes_pool, grouped_tiles, step):
+    quantised = []
+    for g in range(PASSES):
+        codes = codes_pool.tile([P, CHUNK], U32, align_bytes=64)
+        scales = codes_pool.tile([P, CHUNK], U8, align_bytes=64)
+        quantised.append((codes, scales))
+    for first in range(0, CHUNK, step):
+        for g in range(PASSES):
+            codes, scales = quantised[g]
+            nc.vector.quantize_mx(
+                out=codes[:, first : first + step].bitcast(FP8X4),
+                scales=scales[:, first : first + step],
+                in_=grouped_tiles[g][:, first : first + step, :].rearrange("p w t -> p (w t)"),
+            )
+    return quantised
 
 
 def multiply(nc, psum_sums, quantised, w_words, w_planes, channel_tile, block):
@@ -135,6 +143,44 @@ def multiply(nc, psum_sums, quantised, w_words, w_planes, channel_tile, block):
             stop=(g == PASSES - 1),
         )
     return sums
+
+
+def finish_pooled(nc, work, results, psum_turned, identity, biases, pooled, first, count, vector_helps, phi_rows, g_rows, row0):
+    run = count // P
+    pooled_by_channel = work.tile([P, len(POOLED_TILES), POOLED_RUN, P], F32)
+    for k, channel_tile in enumerate(POOLED_TILES):
+        by_run = pooled[:, k, first : first + count].rearrange("c (p t) -> c t p", t=run)
+        if vector_helps and k > 0:
+            nc.vector.tensor_scalar_add(
+                out=pooled_by_channel[:, k, :run], in0=by_run, scalar1=biases[:, channel_tile : channel_tile + 1]
+            )
+        else:
+            nc.scalar.activation(
+                out=pooled_by_channel[:, k, :run],
+                in_=by_run,
+                func=(TANH if k == 0 else IDENTITY),
+                bias=biases[:, channel_tile : channel_tile + 1],
+            )
+    phi_turned = psum_turned.tile([P, POOLED_RUN, P], F32)
+    g_turned = psum_turned.tile([P, POOLED_RUN, 2, P], F32)
+    for t in range(run):
+        nc.tensor.transpose(phi_turned[:, t, :], pooled_by_channel[:, 0, t, :], identity[:])
+        for half_of_g in range(2):
+            nc.tensor.transpose(g_turned[:, t, half_of_g, :], pooled_by_channel[:, 1 + half_of_g, t, :], identity[:])
+    phi = results.tile([P, POOLED_RUN, P], F32)
+    g_out = results.tile([P, POOLED_RUN, 2, P], F32)
+    nc.scalar.copy(out=phi[:, :run], in_=phi_turned[:, :run])
+    if vector_helps:
+        nc.vector.tensor_copy(out=g_out[:, :run], in_=g_turned[:, :run])
+    else:
+        nc.scalar.copy(out=g_out[:, :run], in_=g_turned[:, :run])
+    rows = slice(row0 + first, row0 + first + count)
+    nc.sync.dma_start(
+        out=phi_rows[rows, :].rearrange("(p t) c -> p (t c)", t=run), in_=phi[:, :run].rearrange("p t c -> p (t c)")
+    )
+    nc.sync.dma_start(
+        out=g_rows[rows, :].rearrange("(p t) c -> p (t c)", t=run), in_=g_out[:, :run].rearrange("p t k c -> p (t k c)")
+    )
 
 
 def tile_selfattention3d_pb_t_kernel(
@@ -180,10 +226,15 @@ def tile_selfattention3d_pb_t_kernel(
 
         grouped = [regroup(nc, grouped_pool, raw) for raw in first_raws]
         for i, (b, h) in enumerate(chunks):
-            quantised = [quantise(nc, codes_pool, grouped_g) for grouped_g in grouped]
-            if i + 1 < len(chunks):
+            last_chunk = i == len(chunks) - 1
+            if last_chunk:
+                quantised = quantised_early
+            else:
+                quantised = quantise(nc, codes_pool, grouped, CHUNK)
                 raws = load_chunk(nc, x_pool, x_rows, chunks[i + 1][0], chunks[i + 1][1])
                 grouped = [regroup(nc, grouped_pool, raw) for raw in raws]
+            if i == len(chunks) - 2:
+                quantised_early = quantise(nc, codes_pool, grouped, BLOCK)
 
             pooled = work.tile([P, len(POOLED_TILES), POOLED_CHUNK], F32)
             for block in range(BLOCKS):
@@ -218,31 +269,11 @@ def tile_selfattention3d_pb_t_kernel(
                     out=out_0[b, first : first + BLOCK, :].rearrange("(p t) c -> p (t c)", t=THETA_RUN),
                     in_=theta[:].rearrange("p t c -> p (t c)"),
                 )
-
-            pooled_by_channel = work.tile([P, len(POOLED_TILES), POOLED_RUN, P], F32)
-            for k, channel_tile in enumerate(POOLED_TILES):
-                nc.scalar.activation(
-                    out=pooled_by_channel[:, k],
-                    in_=pooled[:, k, :].rearrange("c (p t) -> c t p", t=POOLED_RUN),
-                    func=(TANH if k == 0 else IDENTITY),
-                    bias=biases[:, channel_tile : channel_tile + 1],
-                )
-            phi_turned = psum_turned.tile([P, POOLED_RUN, P], F32)
-            g_turned = psum_turned.tile([P, POOLED_RUN, 2, P], F32)
-            for t in range(POOLED_RUN):
-                nc.tensor.transpose(phi_turned[:, t, :], pooled_by_channel[:, 0, t, :], identity[:])
-                for half_of_g in range(2):
-                    nc.tensor.transpose(
-                        g_turned[:, t, half_of_g, :], pooled_by_channel[:, 1 + half_of_g, t, :], identity[:]
+                if last_chunk:
+                    finish_pooled(
+                        nc, work, results, psum_turned, identity, biases, pooled,
+                        block * POOLED_BLOCK, POOLED_BLOCK, True, out_1[b], out_2[b], h * POOLED_CHUNK,
                     )
-            phi = results.tile([P, POOLED_RUN * P], F32)
-            g_out = results.tile([P, POOLED_RUN * 2 * P], F32)
-            nc.scalar.copy(out=phi[:], in_=phi_turned[:].rearrange("p t c -> p (t c)"))
-            nc.scalar.copy(out=g_out[:], in_=g_turned[:].rearrange("p t k c -> p (t k c)"))
-            pooled_rows = slice(h * POOLED_CHUNK, (h + 1) * POOLED_CHUNK)
-            nc.sync.dma_start(
-                out=out_1[b, pooled_rows, :].rearrange("(p t) c -> p (t c)", t=POOLED_RUN), in_=phi[:]
-            )
-            nc.sync.dma_start(
-                out=out_2[b, pooled_rows, :].rearrange("(p t) c -> p (t c)", t=POOLED_RUN), in_=g_out[:]
-            )
+
+            if not last_chunk:
+                finish_pooled(nc, work, results, psum_turned, identity, biases, pooled, 0, POOLED_CHUNK, False, out_1[b], out_2[b], h * POOLED_CHUNK)

@@ -70,7 +70,7 @@ def load_biases(nc, consts, psum_turned, identity, b_theta, b_phi, b_g):
     nc.scalar.dma_start(out=rows_bf16[2:4, :], in_=b_g.rearrange("(k c) -> k c", k=2))
     rows = consts.tile([P, P], F32)
     nc.vector.tensor_copy(out=rows[:], in_=rows_bf16[:])
-    columns = psum_turned.tile([P, P], F32, tag="theta_turned")
+    columns = psum_turned.tile([P, P], F32, tag="phi_turned")
     nc.tensor.transpose(columns[:], rows[:], identity[:])
     biases = consts.tile([P, 4], F32)
     nc.vector.tensor_copy(out=biases[:], in_=columns[:, 0:4])
@@ -145,7 +145,7 @@ def multiply(nc, psum_sums, quantised, w_words, w_planes, channel_tile, block):
     return sums
 
 
-def finish_pooled(nc, work, results, psum_turned, identity, biases, pooled, first, count, vector_helps, phi_rows, g_rows, row0):
+def bias_pooled(nc, work, biases, pooled, first, count, vector_helps):
     run = count // P
     pooled_by_channel = work.tile([P, len(POOLED_TILES), POOLED_RUN, P], F32)
     for k, channel_tile in enumerate(POOLED_TILES):
@@ -161,6 +161,11 @@ def finish_pooled(nc, work, results, psum_turned, identity, biases, pooled, firs
                 func=(TANH if k == 0 else IDENTITY),
                 bias=biases[:, channel_tile : channel_tile + 1],
             )
+    return pooled_by_channel
+
+
+def turn_pooled(nc, results, psum_turned, identity, pooled_by_channel, count, vector_helps, phi_rows, g_rows):
+    run = count // P
     phi_turned = psum_turned.tile([P, POOLED_RUN, P], F32)
     g_turned = psum_turned.tile([P, POOLED_RUN, 2, P], F32)
     for t in range(run):
@@ -174,13 +179,29 @@ def finish_pooled(nc, work, results, psum_turned, identity, biases, pooled, firs
         nc.vector.tensor_copy(out=g_out[:, :run], in_=g_turned[:, :run])
     else:
         nc.scalar.copy(out=g_out[:, :run], in_=g_turned[:, :run])
-    rows = slice(row0 + first, row0 + first + count)
+    nc.sync.dma_start(out=phi_rows.rearrange("(p t) c -> p (t c)", t=run), in_=phi[:, :run].rearrange("p t c -> p (t c)"))
     nc.sync.dma_start(
-        out=phi_rows[rows, :].rearrange("(p t) c -> p (t c)", t=run), in_=phi[:, :run].rearrange("p t c -> p (t c)")
+        out=g_rows.rearrange("(p t) c -> p (t c)", t=run), in_=g_out[:, :run].rearrange("p t k c -> p (t k c)")
     )
+
+
+def turn_theta(nc, results, psum_theta, identity, theta_by_channel, theta_rows):
+    theta_turned = psum_theta.tile([P, THETA_RUN, P], F32)
+    for t in range(THETA_RUN):
+        nc.tensor.transpose(theta_turned[:, t, :], theta_by_channel[:, t, :], identity[:])
+    theta = results.tile([P, THETA_RUN, P], F32)
+    nc.scalar.copy(out=theta[:], in_=theta_turned[:])
     nc.sync.dma_start(
-        out=g_rows[rows, :].rearrange("(p t) c -> p (t c)", t=run), in_=g_out[:, :run].rearrange("p t k c -> p (t k c)")
+        out=theta_rows.rearrange("(p t) c -> p (t c)", t=THETA_RUN), in_=theta[:].rearrange("p t c -> p (t c)")
     )
+
+
+def turn_all(nc, results, psum_theta, psum_turned, identity, to_turn):
+    for item in to_turn:
+        if item[0] == "theta":
+            turn_theta(nc, results, psum_theta, identity, item[1], item[2])
+        else:
+            turn_pooled(nc, results, psum_turned, identity, item[1], item[2], item[3], item[4], item[5])
 
 
 def tile_selfattention3d_pb_t_kernel(
@@ -207,9 +228,10 @@ def tile_selfattention3d_pb_t_kernel(
         x_pool = ctx.enter_context(tc.tile_pool(name="x", bufs=8))
         grouped_pool = ctx.enter_context(tc.tile_pool(name="grouped", bufs=4))
         codes_pool = ctx.enter_context(tc.tile_pool(name="codes", bufs=4))
-        work = ctx.enter_context(tc.tile_pool(name="work", bufs=3))
+        work = ctx.enter_context(tc.tile_pool(name="work", bufs=5))
         results = ctx.enter_context(tc.tile_pool(name="results", bufs=3))
-        psum_sums = ctx.enter_context(tc.psum_pool(name="psum_sums", bufs=5))
+        psum_sums = ctx.enter_context(tc.psum_pool(name="psum_sums", bufs=4))
+        psum_theta = ctx.enter_context(tc.psum_pool(name="psum_theta", bufs=2))
         psum_turned = ctx.enter_context(tc.psum_pool(name="psum_turned", bufs=1))
 
         chunks = [(b, h) for b in range(BATCH) for h in range(CHUNKS)]
@@ -225,6 +247,8 @@ def tile_selfattention3d_pb_t_kernel(
         biases = load_biases(nc, consts, psum_turned, identity, b_theta, b_phi, b_g)
 
         grouped = [regroup(nc, grouped_pool, raw) for raw in first_raws]
+        ctx.enter_context(tc.manual_schedule(engines={mybir.EngineType.PE}))
+        to_turn = []
         for i, (b, h) in enumerate(chunks):
             last_chunk = i == len(chunks) - 1
             if last_chunk:
@@ -237,6 +261,7 @@ def tile_selfattention3d_pb_t_kernel(
                 quantised_early = quantise(nc, codes_pool, grouped, BLOCK)
 
             pooled = work.tile([P, len(POOLED_TILES), POOLED_CHUNK], F32)
+            turn_next = []
             for block in range(BLOCKS):
                 for k, channel_tile in enumerate(POOLED_TILES):
                     sums = multiply(nc, psum_sums, quantised, w_words, w_planes, channel_tile, block)
@@ -259,21 +284,19 @@ def tile_selfattention3d_pb_t_kernel(
                     func=TANH,
                     bias=biases[:, THETA : THETA + 1],
                 )
-                theta_turned = psum_turned.tile([P, THETA_RUN, P], F32)
-                for t in range(THETA_RUN):
-                    nc.tensor.transpose(theta_turned[:, t, :], theta_by_channel[:, t, :], identity[:])
-                theta = results.tile([P, THETA_RUN, P], F32)
-                nc.scalar.copy(out=theta[:], in_=theta_turned[:])
                 first = h * CHUNK + block * BLOCK
-                nc.sync.dma_start(
-                    out=out_0[b, first : first + BLOCK, :].rearrange("(p t) c -> p (t c)", t=THETA_RUN),
-                    in_=theta[:].rearrange("p t c -> p (t c)"),
-                )
+                turn_next.append(("theta", theta_by_channel, out_0[b, first : first + BLOCK, :]))
+                if block == 0:
+                    turn_all(nc, results, psum_theta, psum_turned, identity, to_turn)
                 if last_chunk:
-                    finish_pooled(
-                        nc, work, results, psum_turned, identity, biases, pooled,
-                        block * POOLED_BLOCK, POOLED_BLOCK, True, out_1[b], out_2[b], h * POOLED_CHUNK,
-                    )
+                    pooled_by_channel = bias_pooled(nc, work, biases, pooled, block * POOLED_BLOCK, POOLED_BLOCK, True)
+                    rows = slice(h * POOLED_CHUNK + block * POOLED_BLOCK, h * POOLED_CHUNK + (block + 1) * POOLED_BLOCK)
+                    turn_next.append(("pooled", pooled_by_channel, POOLED_BLOCK, True, out_1[b, rows, :], out_2[b, rows, :]))
 
             if not last_chunk:
-                finish_pooled(nc, work, results, psum_turned, identity, biases, pooled, 0, POOLED_CHUNK, False, out_1[b], out_2[b], h * POOLED_CHUNK)
+                pooled_by_channel = bias_pooled(nc, work, biases, pooled, 0, POOLED_CHUNK, False)
+                rows = slice(h * POOLED_CHUNK, (h + 1) * POOLED_CHUNK)
+                turn_next.append(("pooled", pooled_by_channel, POOLED_CHUNK, False, out_1[b, rows, :], out_2[b, rows, :]))
+
+            to_turn = turn_next
+        turn_all(nc, results, psum_theta, psum_turned, identity, to_turn)

@@ -38,8 +38,11 @@ CHUNKS = LOCATIONS // CHUNK
 THETA_RUN = BLOCK // P
 POOLED_RUN = POOLED_CHUNK // P
 
-V_LOCATIONS = 368
+S_LOCATIONS = 496
+V_LOCATIONS = 272
 G_LOCATIONS = 256
+G_OVERLAP = 4
+FIRST_S_LOCATIONS = 344
 
 FLOPS = 2 * BATCH * LOCATIONS * CHANNELS * C_ALL
 
@@ -91,23 +94,42 @@ def load_chunk(nc, x_pool, x_rows, b, h):
     return raws
 
 
-def regroup(nc, grouped_pool, raw):
-    grouped = grouped_pool.tile([P, CHUNK, PACK], BF16, align_bytes=64)
+def regroup(engine_copy, grouped, raw, first, count):
     src = raw[:].rearrange("p t (c i) -> p c t i", i=4)
     dst = grouped[:].rearrange("p (c i) t -> p c t i", i=4)
-    split = V_LOCATIONS // 4
-    last = (CHUNK - G_LOCATIONS) // 4
-    nc.vector.tensor_copy(out=dst[:, :split], in_=src[:, :split])
-    nc.scalar.copy(out=dst[:, split:last], in_=src[:, split:last])
+    engine_copy(out=dst[:, first // 4 : (first + count) // 4], in_=src[:, first // 4 : (first + count) // 4])
+
+
+def regroup_on_gpsimd(nc, grouped, raw):
+    first = CHUNK - G_LOCATIONS - G_OVERLAP
     nc.gpsimd.tensor_scalar(
-        out=grouped[:, CHUNK - G_LOCATIONS :, :],
-        in0=raw[:, :, CHUNK - G_LOCATIONS :].rearrange("p t w -> p w t"),
+        out=grouped[:, first:, :],
+        in0=raw[:, :, first:].rearrange("p t w -> p w t"),
         scalar1=1.0,
         scalar2=0.0,
         op0=MULT,
         op1=ADD,
     )
-    return grouped
+
+
+def products_of_block(nc, psum_sums, work, quantised, w_words, w_planes, biases, pooled, block):
+    for k, channel_tile in enumerate(POOLED_TILES):
+        sums = multiply(nc, psum_sums, quantised, w_words, w_planes, channel_tile, block)
+        nc.vector.tensor_reduce(
+            out=pooled[:, k, block * POOLED_BLOCK : (block + 1) * POOLED_BLOCK].rearrange("c (pair j) -> c pair j", j=SIDE // 2),
+            in_=sums[:].rearrange("c (pair half j side) -> c pair j half side", half=2, j=SIDE // 2, side=2),
+            axis=mybir.AxisListType.XY,
+            op=MAX,
+        )
+    sums = multiply(nc, psum_sums, quantised, w_words, w_planes, THETA, block)
+    theta_by_channel = work.tile([P, THETA_RUN, P], F32)
+    nc.scalar.activation(
+        out=theta_by_channel[:],
+        in_=sums[:].rearrange("c (p t) -> c t p", t=THETA_RUN),
+        func=TANH,
+        bias=biases[:, THETA : THETA + 1],
+    )
+    return theta_by_channel
 
 
 def quantise(nc, codes_pool, grouped_tiles, step):
@@ -145,44 +167,51 @@ def multiply(nc, psum_sums, quantised, w_words, w_planes, channel_tile, block):
     return sums
 
 
-def bias_pooled(nc, work, biases, pooled, first, count, vector_helps):
-    run = count // P
-    pooled_by_channel = work.tile([P, len(POOLED_TILES), POOLED_RUN, P], F32)
-    for k, channel_tile in enumerate(POOLED_TILES):
-        by_run = pooled[:, k, first : first + count].rearrange("c (p t) -> c t p", t=run)
-        if vector_helps and k > 0:
-            nc.vector.tensor_scalar_add(
-                out=pooled_by_channel[:, k, :run], in0=by_run, scalar1=biases[:, channel_tile : channel_tile + 1]
-            )
-        else:
-            nc.scalar.activation(
-                out=pooled_by_channel[:, k, :run],
-                in_=by_run,
-                func=(TANH if k == 0 else IDENTITY),
-                bias=biases[:, channel_tile : channel_tile + 1],
-            )
-    return pooled_by_channel
-
-
-def turn_pooled(nc, results, psum_turned, identity, pooled_by_channel, count, vector_helps, phi_rows, g_rows):
-    run = count // P
+def open_with_biases(nc, psum_turned, ones, bias_rows, count):
+    groups = count // P
     phi_turned = psum_turned.tile([P, POOLED_RUN, P], F32)
     g_turned = psum_turned.tile([P, POOLED_RUN, 2, P], F32)
-    for t in range(run):
-        nc.tensor.transpose(phi_turned[:, t, :], pooled_by_channel[:, 0, t, :], identity[:])
+    nc.tensor.matmul(out=phi_turned[:, :groups], lhsT=ones[:], rhs=bias_rows[:, 0, : groups * P], start=True, stop=False)
+    nc.tensor.matmul(out=g_turned[:, :groups], lhsT=ones[:], rhs=bias_rows[:, 1, : groups * 2 * P], start=True, stop=False)
+    return phi_turned, g_turned
+
+
+def turn_pooled(nc, results, identity, turned, pooled, first, count, vector_helps, phi_rows, g_rows):
+    groups = count // P
+    phi_turned, g_turned = turned
+    for t in range(groups):
+        cols = slice(first + t * P, first + (t + 1) * P)
+        nc.tensor.matmul(
+            out=phi_turned[:, t, :], lhsT=pooled[:, 0, cols], rhs=identity[:], is_transpose=True,
+            start=False, stop=(t == groups - 1),
+        )
+    for t in range(groups):
+        cols = slice(first + t * P, first + (t + 1) * P)
         for half_of_g in range(2):
-            nc.tensor.transpose(g_turned[:, t, half_of_g, :], pooled_by_channel[:, 1 + half_of_g, t, :], identity[:])
+            nc.tensor.matmul(
+                out=g_turned[:, t, half_of_g, :], lhsT=pooled[:, 1 + half_of_g, cols], rhs=identity[:], is_transpose=True,
+                start=False, stop=(t == groups - 1 and half_of_g == 1),
+            )
     phi = results.tile([P, POOLED_RUN, P], F32)
     g_out = results.tile([P, POOLED_RUN, 2, P], F32)
-    nc.scalar.copy(out=phi[:, :run], in_=phi_turned[:, :run])
+    nc.scalar.activation(out=phi[:, :groups], in_=phi_turned[:, :groups], func=TANH)
     if vector_helps:
-        nc.vector.tensor_copy(out=g_out[:, :run], in_=g_turned[:, :run])
+        nc.vector.tensor_copy(out=g_out[:, :groups], in_=g_turned[:, :groups])
     else:
-        nc.scalar.copy(out=g_out[:, :run], in_=g_turned[:, :run])
-    nc.sync.dma_start(out=phi_rows.rearrange("(p t) c -> p (t c)", t=run), in_=phi[:, :run].rearrange("p t c -> p (t c)"))
+        nc.scalar.copy(out=g_out[:, :groups], in_=g_turned[:, :groups])
+    nc.sync.dma_start(out=phi_rows.rearrange("(t p) c -> p t c", t=groups), in_=phi[:, :groups])
     nc.sync.dma_start(
-        out=g_rows.rearrange("(p t) c -> p (t c)", t=run), in_=g_out[:, :run].rearrange("p t k c -> p (t k c)")
+        out=g_rows.rearrange("(t p) c -> p t c", t=groups), in_=g_out[:, :groups].rearrange("p t k c -> p t (k c)")
     )
+
+
+def load_bias_rows(nc, consts, b_phi, b_g):
+    bias_rows = consts.tile([P, 2, 4 * P], BF16)
+    nc.vector.memset(bias_rows[:], 0.0)
+    for t in range(POOLED_RUN):
+        nc.scalar.dma_start(out=bias_rows[0:1, 0, t * P : (t + 1) * P], in_=b_phi.rearrange("(k c) -> k c", k=1))
+        nc.scalar.dma_start(out=bias_rows[0:1, 1, t * 2 * P : (t + 1) * 2 * P], in_=b_g.rearrange("(k c) -> k c", k=1))
+    return bias_rows
 
 
 def turn_theta(nc, results, psum_theta, identity, theta_by_channel, theta_rows):
@@ -196,12 +225,19 @@ def turn_theta(nc, results, psum_theta, identity, theta_by_channel, theta_rows):
     )
 
 
-def turn_all(nc, results, psum_theta, psum_turned, identity, to_turn):
+def turn_all(nc, results, psum_theta, psum_turned, identity, ones, bias_rows, to_turn):
+    turned = None
+    pooled_entries = [item for item in to_turn if item[0] == "pooled"]
+    if pooled_entries:
+        turned = open_with_biases(nc, psum_turned, ones, bias_rows, pooled_entries[0][3])
     for item in to_turn:
         if item[0] == "theta":
             turn_theta(nc, results, psum_theta, identity, item[1], item[2])
         else:
-            turn_pooled(nc, results, psum_turned, identity, item[1], item[2], item[3], item[4], item[5])
+            if turned is None:
+                turned = open_with_biases(nc, psum_turned, ones, bias_rows, item[3])
+            turn_pooled(nc, results, identity, turned, item[1], item[2], item[3], item[4], item[5], item[6])
+            turned = None
 
 
 def tile_selfattention3d_pb_t_kernel(
@@ -235,68 +271,72 @@ def tile_selfattention3d_pb_t_kernel(
         psum_turned = ctx.enter_context(tc.psum_pool(name="psum_turned", bufs=1))
 
         chunks = [(b, h) for b in range(BATCH) for h in range(CHUNKS)]
+        ahead = 4
 
-        first_raws = load_chunk(nc, x_pool, x_rows, chunks[0][0], chunks[0][1])
+        raws = {0: load_chunk(nc, x_pool, x_rows, chunks[0][0], chunks[0][1])}
         w_words, w_planes = load_weights(
             nc,
             consts,
             [(w_theta_words, w_theta_scales, 0, 128), (w_phi_words, w_phi_scales, 128, 128), (w_g_words, w_g_scales, 256, 256)],
         )
+        for i in range(1, ahead):
+            raws[i] = load_chunk(nc, x_pool, x_rows, chunks[i][0], chunks[i][1])
         identity = consts.tile([P, P], F32)
         make_identity(nc, identity[:])
         biases = load_biases(nc, consts, psum_turned, identity, b_theta, b_phi, b_g)
+        bias_rows = load_bias_rows(nc, consts, b_phi, b_g)
+        ones = consts.tile([P, P], BF16)
+        nc.vector.memset(ones[:], 1.0)
 
-        grouped = [regroup(nc, grouped_pool, raw) for raw in first_raws]
-        ctx.enter_context(tc.manual_schedule(engines={mybir.EngineType.PE}))
+        ctx.enter_context(
+            tc.manual_schedule(
+                engines={mybir.EngineType.PE, mybir.EngineType.DVE, mybir.EngineType.Activation, mybir.EngineType.Pool}
+            )
+        )
+        grouped = []
+        for g in range(PASSES):
+            grouped_g = grouped_pool.tile([P, CHUNK, PACK], BF16, align_bytes=64, tag="grouped")
+            regroup(nc.scalar.copy, grouped_g, raws[0][g], 0, FIRST_S_LOCATIONS)
+            regroup(nc.vector.tensor_copy, grouped_g, raws[0][g], FIRST_S_LOCATIONS, CHUNK - FIRST_S_LOCATIONS)
+            grouped.append(grouped_g)
+
         to_turn = []
         for i, (b, h) in enumerate(chunks):
             last_chunk = i == len(chunks) - 1
-            if last_chunk:
-                quantised = quantised_early
-            else:
-                quantised = quantise(nc, codes_pool, grouped, CHUNK)
-                raws = load_chunk(nc, x_pool, x_rows, chunks[i + 1][0], chunks[i + 1][1])
-                grouped = [regroup(nc, grouped_pool, raw) for raw in raws]
-            if i == len(chunks) - 2:
-                quantised_early = quantise(nc, codes_pool, grouped, BLOCK)
+            quantised = quantise(nc, codes_pool, grouped, BLOCK if last_chunk else CHUNK)
+            if i + ahead < len(chunks):
+                raws[i + ahead] = load_chunk(nc, x_pool, x_rows, chunks[i + ahead][0], chunks[i + ahead][1])
+            if not last_chunk:
+                grouped = []
+                for g in range(PASSES):
+                    grouped_g = grouped_pool.tile([P, CHUNK, PACK], BF16, align_bytes=64, tag="grouped")
+                    regroup(nc.vector.tensor_copy, grouped_g, raws[i + 1][g], S_LOCATIONS, V_LOCATIONS)
+                    grouped.append(grouped_g)
+                for g in reversed(range(PASSES)):
+                    regroup_on_gpsimd(nc, grouped[g], raws[i + 1][g])
 
             pooled = work.tile([P, len(POOLED_TILES), POOLED_CHUNK], F32)
             turn_next = []
             for block in range(BLOCKS):
-                for k, channel_tile in enumerate(POOLED_TILES):
-                    sums = multiply(nc, psum_sums, quantised, w_words, w_planes, channel_tile, block)
-                    nc.vector.tensor_reduce(
-                        out=pooled[:, k, block * POOLED_BLOCK : (block + 1) * POOLED_BLOCK].rearrange(
-                            "c (pair j) -> c pair j", j=SIDE // 2
-                        ),
-                        in_=sums[:].rearrange(
-                            "c (pair half j side) -> c pair j half side", half=2, j=SIDE // 2, side=2
-                        ),
-                        axis=mybir.AxisListType.XY,
-                        op=MAX,
-                    )
-
-                sums = multiply(nc, psum_sums, quantised, w_words, w_planes, THETA, block)
-                theta_by_channel = work.tile([P, THETA_RUN, P], F32)
-                nc.scalar.activation(
-                    out=theta_by_channel[:],
-                    in_=sums[:].rearrange("c (p t) -> c t p", t=THETA_RUN),
-                    func=TANH,
-                    bias=biases[:, THETA : THETA + 1],
+                if not last_chunk:
+                    regroup(nc.scalar.copy, grouped[block], raws[i + 1][block], 0, S_LOCATIONS)
+                theta_by_channel = products_of_block(
+                    nc, psum_sums, work, quantised, w_words, w_planes, biases, pooled, block
                 )
                 first = h * CHUNK + block * BLOCK
                 turn_next.append(("theta", theta_by_channel, out_0[b, first : first + BLOCK, :]))
-                if block == 0:
-                    turn_all(nc, results, psum_theta, psum_turned, identity, to_turn)
                 if last_chunk:
-                    pooled_by_channel = bias_pooled(nc, work, biases, pooled, block * POOLED_BLOCK, POOLED_BLOCK, True)
                     rows = slice(h * POOLED_CHUNK + block * POOLED_BLOCK, h * POOLED_CHUNK + (block + 1) * POOLED_BLOCK)
-                    turn_next.append(("pooled", pooled_by_channel, POOLED_BLOCK, True, out_1[b, rows, :], out_2[b, rows, :]))
+                    turn_next.append(
+                        ("pooled", pooled, block * POOLED_BLOCK, POOLED_BLOCK, True, out_1[b, rows, :], out_2[b, rows, :])
+                    )
+                    if block == 0:
+                        turn_all(nc, results, psum_theta, psum_turned, identity, ones, bias_rows, to_turn)
 
             if not last_chunk:
-                pooled_by_channel = bias_pooled(nc, work, biases, pooled, 0, POOLED_CHUNK, False)
                 rows = slice(h * POOLED_CHUNK, (h + 1) * POOLED_CHUNK)
-                turn_next.append(("pooled", pooled_by_channel, POOLED_CHUNK, False, out_1[b, rows, :], out_2[b, rows, :]))
+                turn_next.append(("pooled", pooled, 0, POOLED_CHUNK, False, out_1[b, rows, :], out_2[b, rows, :]))
+                turn_all(nc, results, psum_theta, psum_turned, identity, ones, bias_rows, to_turn)
 
             to_turn = turn_next
-        turn_all(nc, results, psum_theta, psum_turned, identity, to_turn)
+        turn_all(nc, results, psum_theta, psum_turned, identity, ones, bias_rows, to_turn)

@@ -303,7 +303,7 @@ def tile_selfattention3d_pb_t_kernel(
         to_turn = []
         for i, (b, h) in enumerate(chunks):
             last_chunk = i == len(chunks) - 1
-            quantised = quantise(nc, codes_pool, grouped, BLOCK if last_chunk else CHUNK)
+            quantised = quantise(nc, codes_pool, grouped, BLOCK)
             if i + ahead < len(chunks):
                 raws[i + ahead] = load_chunk(nc, x_pool, x_rows, chunks[i + ahead][0], chunks[i + ahead][1])
             if not last_chunk:

@@ -38,8 +38,8 @@ CHUNKS = LOCATIONS // CHUNK
 THETA_RUN = BLOCK // P
 POOLED_RUN = POOLED_CHUNK // P
 
-S_LOCATIONS = 496
-V_LOCATIONS = 272
+S_LOCATIONS = 472
+V_LOCATIONS = 296
 G_LOCATIONS = 256
 G_OVERLAP = 4
 FIRST_S_LOCATIONS = 344

@@ -13,7 +13,6 @@ MAX = mybir.AluOpType.max
 MULT = mybir.AluOpType.mult
 ADD = mybir.AluOpType.add
 TANH = mybir.ActivationFunctionType.Tanh
-IDENTITY = mybir.ActivationFunctionType.Identity
 
 P = 128
 PACK = 4
@@ -29,18 +28,18 @@ C_ALL = 512
 THETA = 0
 POOLED_TILES = (1, 2, 3)
 
-BLOCK = 512
-POOLED_BLOCK = BLOCK // 4
-BLOCKS = 2
-CHUNK = BLOCKS * BLOCK
+LOAD = 512
+POOLED_LOAD = LOAD // 4
+LOADS = 2
+CHUNK = LOADS * LOAD
 POOLED_CHUNK = CHUNK // 4
 CHUNKS = LOCATIONS // CHUNK
-THETA_RUN = BLOCK // P
-POOLED_RUN = POOLED_CHUNK // P
+THETA_RUN = LOAD // P
+AHEAD = 4
 
-S_LOCATIONS = 472
-V_LOCATIONS = 296
-G_LOCATIONS = 256
+S_LOCATIONS = 448
+V_LOCATIONS = 288
+G_LOCATIONS = 288
 G_OVERLAP = 4
 FIRST_S_LOCATIONS = 344
 
@@ -49,8 +48,8 @@ FLOPS = 2 * BATCH * LOCATIONS * CHANNELS * C_ALL
 
 def load_weights(nc, consts, weights):
     w_words = consts.tile([P, PASSES, C_ALL], U32, align_bytes=64)
-    w_planes = consts.tile([P, PASSES, C_ALL], U8, align_bytes=64)
-    nc.vector.memset(w_planes[:].bitcast(I32), 0)
+    w_scales = consts.tile([P, PASSES, C_ALL], U8, align_bytes=64)
+    nc.vector.memset(w_scales[:].bitcast(I32), 0)
     for words, scales, first, count in weights:
         cols = slice(first, first + count)
         nc.sync.dma_start(
@@ -59,28 +58,36 @@ def load_weights(nc, consts, weights):
         )
         for quadrant in range(4):
             nc.sync.dma_start(
-                out=w_planes[32 * quadrant : 32 * quadrant + 4, :, cols].bitcast(I32),
+                out=w_scales[32 * quadrant : 32 * quadrant + 4, :, cols].bitcast(I32),
                 in_=scales[:, 4 * quadrant : 4 * quadrant + 4, :].rearrange("g r n -> r g n").bitcast(I32),
             )
-    return w_words, w_planes
+    return w_words, w_scales
 
 
-def load_biases(nc, consts, psum_turned, identity, b_theta, b_phi, b_g):
+def load_theta_bias(nc, consts, psum_turned, identity, b_theta):
     rows_bf16 = consts.tile([P, P], BF16)
     nc.vector.memset(rows_bf16[:], 0.0)
     nc.scalar.dma_start(out=rows_bf16[0:1, :], in_=b_theta.rearrange("(k c) -> k c", k=1))
-    nc.scalar.dma_start(out=rows_bf16[1:2, :], in_=b_phi.rearrange("(k c) -> k c", k=1))
-    nc.scalar.dma_start(out=rows_bf16[2:4, :], in_=b_g.rearrange("(k c) -> k c", k=2))
     rows = consts.tile([P, P], F32)
     nc.vector.tensor_copy(out=rows[:], in_=rows_bf16[:])
     columns = psum_turned.tile([P, P], F32, tag="phi_turned")
     nc.tensor.transpose(columns[:], rows[:], identity[:])
-    biases = consts.tile([P, 4], F32)
-    nc.vector.tensor_copy(out=biases[:], in_=columns[:, 0:4])
-    return biases
+    theta_bias = consts.tile([P, 1], F32)
+    nc.vector.tensor_copy(out=theta_bias[:], in_=columns[:, 0:1])
+    return theta_bias
 
 
-def load_chunk(nc, x_pool, x_rows, b, h):
+def load_bias_rows(nc, consts, b_phi, b_g):
+    bias_rows = consts.tile([P, 2, 4 * P], BF16)
+    nc.vector.memset(bias_rows[:], 0.0)
+    for t in range(LOADS):
+        nc.scalar.dma_start(out=bias_rows[0:1, 0, t * P : (t + 1) * P], in_=b_phi.rearrange("(k c) -> k c", k=1))
+        nc.scalar.dma_start(out=bias_rows[0:1, 1, t * 2 * P : (t + 1) * 2 * P], in_=b_g.rearrange("(k c) -> k c", k=1))
+    return bias_rows
+
+
+def load_chunk(nc, x_pool, x_rows, chunk):
+    b, h = chunk
     raws = []
     for g in range(PASSES):
         raw = x_pool.tile([P, PACK, CHUNK], BF16)
@@ -112,53 +119,33 @@ def regroup_on_gpsimd(nc, grouped, raw):
     )
 
 
-def products_of_block(nc, psum_sums, work, quantised, w_words, w_planes, biases, pooled, block):
-    for k, channel_tile in enumerate(POOLED_TILES):
-        sums = multiply(nc, psum_sums, quantised, w_words, w_planes, channel_tile, block)
-        nc.vector.tensor_reduce(
-            out=pooled[:, k, block * POOLED_BLOCK : (block + 1) * POOLED_BLOCK].rearrange("c (pair j) -> c pair j", j=SIDE // 2),
-            in_=sums[:].rearrange("c (pair half j side) -> c pair j half side", half=2, j=SIDE // 2, side=2),
-            axis=mybir.AxisListType.XY,
-            op=MAX,
-        )
-    sums = multiply(nc, psum_sums, quantised, w_words, w_planes, THETA, block)
-    theta_by_channel = work.tile([P, THETA_RUN, P], F32)
-    nc.scalar.activation(
-        out=theta_by_channel[:],
-        in_=sums[:].rearrange("c (p t) -> c t p", t=THETA_RUN),
-        func=TANH,
-        bias=biases[:, THETA : THETA + 1],
-    )
-    return theta_by_channel
-
-
-def quantise(nc, codes_pool, grouped_tiles, step):
+def quantise(nc, codes_pool, grouped):
     quantised = []
     for g in range(PASSES):
         codes = codes_pool.tile([P, CHUNK], U32, align_bytes=64)
         scales = codes_pool.tile([P, CHUNK], U8, align_bytes=64)
         quantised.append((codes, scales))
-    for first in range(0, CHUNK, step):
+    for first in range(0, CHUNK, LOAD):
         for g in range(PASSES):
             codes, scales = quantised[g]
             nc.vector.quantize_mx(
-                out=codes[:, first : first + step].bitcast(FP8X4),
-                scales=scales[:, first : first + step],
-                in_=grouped_tiles[g][:, first : first + step, :].rearrange("p w t -> p (w t)"),
+                out=codes[:, first : first + LOAD].bitcast(FP8X4),
+                scales=scales[:, first : first + LOAD],
+                in_=grouped[g][:, first : first + LOAD, :].rearrange("p w t -> p (w t)"),
             )
     return quantised
 
 
-def multiply(nc, psum_sums, quantised, w_words, w_planes, channel_tile, block):
+def multiply(nc, psum_sums, quantised, w_words, w_scales, channel_tile, load):
     w_cols = slice(channel_tile * P, (channel_tile + 1) * P)
-    x_cols = slice(block * BLOCK, (block + 1) * BLOCK)
-    sums = psum_sums.tile([P, BLOCK], F32)
+    x_cols = slice(load * LOAD, (load + 1) * LOAD)
+    sums = psum_sums.tile([P, LOAD], F32)
     for g in range(PASSES):
         codes, scales = quantised[g]
         nc.tensor.matmul_mx(
             out=sums[:],
             lhsT=w_words[:, g, w_cols].bitcast(FP8X4),
-            lhsT_scale=w_planes[:, g, w_cols],
+            lhsT_scale=w_scales[:, g, w_cols],
             rhs=codes[:, x_cols].bitcast(FP8X4),
             rhs_scale=scales[:, x_cols],
             start=(g == 0),
@@ -167,17 +154,35 @@ def multiply(nc, psum_sums, quantised, w_words, w_planes, channel_tile, block):
     return sums
 
 
-def open_with_biases(nc, psum_turned, ones, bias_rows, count):
-    groups = count // P
-    phi_turned = psum_turned.tile([P, POOLED_RUN, P], F32)
-    g_turned = psum_turned.tile([P, POOLED_RUN, 2, P], F32)
+def products(nc, psum_sums, work, quantised, w_words, w_scales, theta_bias, pooled, load):
+    for k, channel_tile in enumerate(POOLED_TILES):
+        sums = multiply(nc, psum_sums, quantised, w_words, w_scales, channel_tile, load)
+        nc.vector.tensor_reduce(
+            out=pooled[:, k, load * POOLED_LOAD : (load + 1) * POOLED_LOAD].rearrange("c (pair j) -> c pair j", j=SIDE // 2),
+            in_=sums[:].rearrange("c (pair half j side) -> c pair j half side", half=2, j=SIDE // 2, side=2),
+            axis=mybir.AxisListType.XY,
+            op=MAX,
+        )
+    sums = multiply(nc, psum_sums, quantised, w_words, w_scales, THETA, load)
+    theta_by_channel = work.tile([P, THETA_RUN, P], F32)
+    nc.scalar.activation(
+        out=theta_by_channel[:],
+        in_=sums[:].rearrange("c (p t) -> c t p", t=THETA_RUN),
+        func=TANH,
+        bias=theta_bias[:],
+    )
+    return theta_by_channel
+
+
+def open_with_biases(nc, psum_turned, ones, bias_rows, groups):
+    phi_turned = psum_turned.tile([P, LOADS, P], F32)
+    g_turned = psum_turned.tile([P, LOADS, 2, P], F32)
     nc.tensor.matmul(out=phi_turned[:, :groups], lhsT=ones[:], rhs=bias_rows[:, 0, : groups * P], start=True, stop=False)
     nc.tensor.matmul(out=g_turned[:, :groups], lhsT=ones[:], rhs=bias_rows[:, 1, : groups * 2 * P], start=True, stop=False)
     return phi_turned, g_turned
 
 
-def turn_pooled(nc, results, identity, turned, pooled, first, count, vector_helps, phi_rows, g_rows):
-    groups = count // P
+def turn_pooled(nc, results, identity, turned, pooled, first, groups, g_copy, phi_rows, g_rows):
     phi_turned, g_turned = turned
     for t in range(groups):
         cols = slice(first + t * P, first + (t + 1) * P)
@@ -192,26 +197,14 @@ def turn_pooled(nc, results, identity, turned, pooled, first, count, vector_help
                 out=g_turned[:, t, half_of_g, :], lhsT=pooled[:, 1 + half_of_g, cols], rhs=identity[:], is_transpose=True,
                 start=False, stop=(t == groups - 1 and half_of_g == 1),
             )
-    phi = results.tile([P, POOLED_RUN, P], F32)
-    g_out = results.tile([P, POOLED_RUN, 2, P], F32)
+    phi = results.tile([P, LOADS, P], F32)
+    g_out = results.tile([P, LOADS, 2, P], F32)
     nc.scalar.activation(out=phi[:, :groups], in_=phi_turned[:, :groups], func=TANH)
-    if vector_helps:
-        nc.vector.tensor_copy(out=g_out[:, :groups], in_=g_turned[:, :groups])
-    else:
-        nc.scalar.copy(out=g_out[:, :groups], in_=g_turned[:, :groups])
+    g_copy(out=g_out[:, :groups], in_=g_turned[:, :groups])
     nc.sync.dma_start(out=phi_rows.rearrange("(t p) c -> p t c", t=groups), in_=phi[:, :groups])
     nc.sync.dma_start(
         out=g_rows.rearrange("(t p) c -> p t c", t=groups), in_=g_out[:, :groups].rearrange("p t k c -> p t (k c)")
     )
-
-
-def load_bias_rows(nc, consts, b_phi, b_g):
-    bias_rows = consts.tile([P, 2, 4 * P], BF16)
-    nc.vector.memset(bias_rows[:], 0.0)
-    for t in range(POOLED_RUN):
-        nc.scalar.dma_start(out=bias_rows[0:1, 0, t * P : (t + 1) * P], in_=b_phi.rearrange("(k c) -> k c", k=1))
-        nc.scalar.dma_start(out=bias_rows[0:1, 1, t * 2 * P : (t + 1) * 2 * P], in_=b_g.rearrange("(k c) -> k c", k=1))
-    return bias_rows
 
 
 def turn_theta(nc, results, psum_theta, identity, theta_by_channel, theta_rows):
@@ -223,21 +216,6 @@ def turn_theta(nc, results, psum_theta, identity, theta_by_channel, theta_rows):
     nc.sync.dma_start(
         out=theta_rows.rearrange("(p t) c -> p (t c)", t=THETA_RUN), in_=theta[:].rearrange("p t c -> p (t c)")
     )
-
-
-def turn_all(nc, results, psum_theta, psum_turned, identity, ones, bias_rows, to_turn):
-    turned = None
-    pooled_entries = [item for item in to_turn if item[0] == "pooled"]
-    if pooled_entries:
-        turned = open_with_biases(nc, psum_turned, ones, bias_rows, pooled_entries[0][3])
-    for item in to_turn:
-        if item[0] == "theta":
-            turn_theta(nc, results, psum_theta, identity, item[1], item[2])
-        else:
-            if turned is None:
-                turned = open_with_biases(nc, psum_turned, ones, bias_rows, item[3])
-            turn_pooled(nc, results, identity, turned, item[1], item[2], item[3], item[4], item[5], item[6])
-            turned = None
 
 
 def tile_selfattention3d_pb_t_kernel(
@@ -261,9 +239,9 @@ def tile_selfattention3d_pb_t_kernel(
 
     with ExitStack() as ctx:
         consts = ctx.enter_context(tc.tile_pool(name="consts", bufs=1))
-        x_pool = ctx.enter_context(tc.tile_pool(name="x", bufs=8))
-        grouped_pool = ctx.enter_context(tc.tile_pool(name="grouped", bufs=4))
-        codes_pool = ctx.enter_context(tc.tile_pool(name="codes", bufs=4))
+        x_pool = ctx.enter_context(tc.tile_pool(name="x", bufs=AHEAD * PASSES))
+        grouped_pool = ctx.enter_context(tc.tile_pool(name="grouped", bufs=2 * PASSES))
+        codes_pool = ctx.enter_context(tc.tile_pool(name="codes", bufs=2 * PASSES))
         work = ctx.enter_context(tc.tile_pool(name="work", bufs=5))
         results = ctx.enter_context(tc.tile_pool(name="results", bufs=3))
         psum_sums = ctx.enter_context(tc.psum_pool(name="psum_sums", bufs=4))
@@ -271,22 +249,48 @@ def tile_selfattention3d_pb_t_kernel(
         psum_turned = ctx.enter_context(tc.psum_pool(name="psum_turned", bufs=1))
 
         chunks = [(b, h) for b in range(BATCH) for h in range(CHUNKS)]
-        ahead = 4
 
-        raws = {0: load_chunk(nc, x_pool, x_rows, chunks[0][0], chunks[0][1])}
-        w_words, w_planes = load_weights(
+        raws = {0: load_chunk(nc, x_pool, x_rows, chunks[0])}
+        warm = consts.tile([P, 1], F32)
+        nc.vector.memset(warm[:], 0.0)
+        nc.scalar.activation(out=warm[:], in_=warm[:], func=TANH)
+        w_words, w_scales = load_weights(
             nc,
             consts,
             [(w_theta_words, w_theta_scales, 0, 128), (w_phi_words, w_phi_scales, 128, 128), (w_g_words, w_g_scales, 256, 256)],
         )
-        for i in range(1, ahead):
-            raws[i] = load_chunk(nc, x_pool, x_rows, chunks[i][0], chunks[i][1])
+        for i in range(1, AHEAD):
+            raws[i] = load_chunk(nc, x_pool, x_rows, chunks[i])
         identity = consts.tile([P, P], F32)
         make_identity(nc, identity[:])
-        biases = load_biases(nc, consts, psum_turned, identity, b_theta, b_phi, b_g)
+        theta_bias = load_theta_bias(nc, consts, psum_turned, identity, b_theta)
         bias_rows = load_bias_rows(nc, consts, b_phi, b_g)
         ones = consts.tile([P, P], BF16)
         nc.vector.memset(ones[:], 1.0)
+
+        def finish(chunk, thetas, pooled, by_load):
+            b, h = chunk
+            theta_rows = [out_0[b, h * CHUNK + load * LOAD : h * CHUNK + (load + 1) * LOAD, :] for load in range(LOADS)]
+            if by_load:
+                for load in range(LOADS):
+                    rows = slice(h * POOLED_CHUNK + load * POOLED_LOAD, h * POOLED_CHUNK + (load + 1) * POOLED_LOAD)
+                    if load == 0:
+                        turned = open_with_biases(nc, psum_turned, ones, bias_rows, 1)
+                    turn_theta(nc, results, psum_theta, identity, thetas[load], theta_rows[load])
+                    if load > 0:
+                        turned = open_with_biases(nc, psum_turned, ones, bias_rows, 1)
+                    turn_pooled(
+                        nc, results, identity, turned, pooled, load * POOLED_LOAD, 1, nc.vector.tensor_copy,
+                        out_1[b, rows, :], out_2[b, rows, :],
+                    )
+            else:
+                rows = slice(h * POOLED_CHUNK, (h + 1) * POOLED_CHUNK)
+                turned = open_with_biases(nc, psum_turned, ones, bias_rows, LOADS)
+                for load in range(LOADS):
+                    turn_theta(nc, results, psum_theta, identity, thetas[load], theta_rows[load])
+                turn_pooled(
+                    nc, results, identity, turned, pooled, 0, LOADS, nc.scalar.copy, out_1[b, rows, :], out_2[b, rows, :]
+                )
 
         ctx.enter_context(
             tc.manual_schedule(
@@ -300,12 +304,12 @@ def tile_selfattention3d_pb_t_kernel(
             regroup(nc.vector.tensor_copy, grouped_g, raws[0][g], FIRST_S_LOCATIONS, CHUNK - FIRST_S_LOCATIONS)
             grouped.append(grouped_g)
 
-        to_turn = []
-        for i, (b, h) in enumerate(chunks):
+        waiting = None
+        for i, chunk in enumerate(chunks):
             last_chunk = i == len(chunks) - 1
-            quantised = quantise(nc, codes_pool, grouped, BLOCK)
-            if i + ahead < len(chunks):
-                raws[i + ahead] = load_chunk(nc, x_pool, x_rows, chunks[i + ahead][0], chunks[i + ahead][1])
+            quantised = quantise(nc, codes_pool, grouped)
+            if i + AHEAD < len(chunks):
+                raws[i + AHEAD] = load_chunk(nc, x_pool, x_rows, chunks[i + AHEAD])
             if not last_chunk:
                 grouped = []
                 for g in range(PASSES):
@@ -316,27 +320,14 @@ def tile_selfattention3d_pb_t_kernel(
                     regroup_on_gpsimd(nc, grouped[g], raws[i + 1][g])
 
             pooled = work.tile([P, len(POOLED_TILES), POOLED_CHUNK], F32)
-            turn_next = []
-            for block in range(BLOCKS):
+            thetas = []
+            for load in range(LOADS):
                 if not last_chunk:
-                    regroup(nc.scalar.copy, grouped[block], raws[i + 1][block], 0, S_LOCATIONS)
-                theta_by_channel = products_of_block(
-                    nc, psum_sums, work, quantised, w_words, w_planes, biases, pooled, block
-                )
-                first = h * CHUNK + block * BLOCK
-                turn_next.append(("theta", theta_by_channel, out_0[b, first : first + BLOCK, :]))
-                if last_chunk:
-                    rows = slice(h * POOLED_CHUNK + block * POOLED_BLOCK, h * POOLED_CHUNK + (block + 1) * POOLED_BLOCK)
-                    turn_next.append(
-                        ("pooled", pooled, block * POOLED_BLOCK, POOLED_BLOCK, True, out_1[b, rows, :], out_2[b, rows, :])
-                    )
-                    if block == 0:
-                        turn_all(nc, results, psum_theta, psum_turned, identity, ones, bias_rows, to_turn)
-
-            if not last_chunk:
-                rows = slice(h * POOLED_CHUNK, (h + 1) * POOLED_CHUNK)
-                turn_next.append(("pooled", pooled, 0, POOLED_CHUNK, False, out_1[b, rows, :], out_2[b, rows, :]))
-                turn_all(nc, results, psum_theta, psum_turned, identity, ones, bias_rows, to_turn)
-
-            to_turn = turn_next
-        turn_all(nc, results, psum_theta, psum_turned, identity, ones, bias_rows, to_turn)
+                    regroup(nc.scalar.copy, grouped[load], raws[i + 1][load], 0, S_LOCATIONS)
+                thetas.append(products(nc, psum_sums, work, quantised, w_words, w_scales, theta_bias, pooled, load))
+                if last_chunk and load == 0:
+                    finish(waiting[0], waiting[1], waiting[2], False)
+            if waiting is not None and not last_chunk:
+                finish(waiting[0], waiting[1], waiting[2], False)
+            waiting = (chunk, thetas, pooled)
+        finish(waiting[0], waiting[1], waiting[2], True)

@@ -46,34 +46,24 @@ FIRST_S_LOCATIONS = 344
 FLOPS = 2 * BATCH * LOCATIONS * CHANNELS * C_ALL
 
 
-def load_weights(nc, consts, weights):
-    w_words = consts.tile([P, PASSES, C_ALL], U32, align_bytes=64)
-    w_scales = consts.tile([P, PASSES, C_ALL], U8, align_bytes=64)
-    nc.vector.memset(w_scales[:].bitcast(I32), 0)
-    for words, scales, first, count in weights:
-        cols = slice(first, first + count)
+def load_words(nc, w_words, words, cols):
+    nc.sync.dma_start(
+        out=w_words[:, :, cols].bitcast(I32),
+        in_=words.rearrange("g p n t -> p g (n t)").bitcast(I32),
+    )
+
+
+def load_scales(nc, w_scales, scales, cols):
+    for quadrant in range(4):
         nc.sync.dma_start(
-            out=w_words[:, :, cols].bitcast(I32),
-            in_=words.rearrange("g p n t -> p g (n t)").bitcast(I32),
+            out=w_scales[32 * quadrant : 32 * quadrant + 4, :, cols].bitcast(I32),
+            in_=scales[:, 4 * quadrant : 4 * quadrant + 4, :].rearrange("g r n -> r g n").bitcast(I32),
         )
-        for quadrant in range(4):
-            nc.sync.dma_start(
-                out=w_scales[32 * quadrant : 32 * quadrant + 4, :, cols].bitcast(I32),
-                in_=scales[:, 4 * quadrant : 4 * quadrant + 4, :].rearrange("g r n -> r g n").bitcast(I32),
-            )
-    return w_words, w_scales
 
 
-def load_theta_bias(nc, consts, psum_turned, identity, b_theta):
-    rows_bf16 = consts.tile([P, P], BF16)
-    nc.vector.memset(rows_bf16[:], 0.0)
-    nc.scalar.dma_start(out=rows_bf16[0:1, :], in_=b_theta.rearrange("(k c) -> k c", k=1))
-    rows = consts.tile([P, P], F32)
-    nc.vector.tensor_copy(out=rows[:], in_=rows_bf16[:])
-    columns = psum_turned.tile([P, P], F32, tag="phi_turned")
-    nc.tensor.transpose(columns[:], rows[:], identity[:])
-    theta_bias = consts.tile([P, 1], F32)
-    nc.vector.tensor_copy(out=theta_bias[:], in_=columns[:, 0:1])
+def load_theta_bias(nc, consts, b_theta):
+    theta_bias = consts.tile([P, 1], BF16)
+    nc.gpsimd.dma_start(out=theta_bias[:], in_=b_theta.rearrange("(p c) -> p c", c=1))
     return theta_bias
 
 
@@ -81,17 +71,17 @@ def load_bias_rows(nc, consts, b_phi, b_g):
     bias_rows = consts.tile([P, 2, 4 * P], BF16)
     nc.vector.memset(bias_rows[:], 0.0)
     for t in range(LOADS):
-        nc.scalar.dma_start(out=bias_rows[0:1, 0, t * P : (t + 1) * P], in_=b_phi.rearrange("(k c) -> k c", k=1))
-        nc.scalar.dma_start(out=bias_rows[0:1, 1, t * 2 * P : (t + 1) * 2 * P], in_=b_g.rearrange("(k c) -> k c", k=1))
+        nc.gpsimd.dma_start(out=bias_rows[0:1, 0, t * P : (t + 1) * P], in_=b_phi.rearrange("(k c) -> k c", k=1))
+        nc.gpsimd.dma_start(out=bias_rows[0:1, 1, t * 2 * P : (t + 1) * 2 * P], in_=b_g.rearrange("(k c) -> k c", k=1))
     return bias_rows
 
 
-def load_chunk(nc, x_pool, x_rows, chunk):
+def load_chunk(queue, x_pool, x_rows, chunk):
     b, h = chunk
     raws = []
     for g in range(PASSES):
         raw = x_pool.tile([P, PACK, CHUNK], BF16)
-        nc.sync.dma_start(
+        queue.dma_start(
             out=raw[:],
             in_=x_rows[b, g * K_PASS : (g + 1) * K_PASS, h * CHUNK : (h + 1) * CHUNK].rearrange(
                 "(p t) w -> p t w", t=PACK
@@ -250,20 +240,25 @@ def tile_selfattention3d_pb_t_kernel(
 
         chunks = [(b, h) for b in range(BATCH) for h in range(CHUNKS)]
 
-        raws = {0: load_chunk(nc, x_pool, x_rows, chunks[0])}
+        raws = {0: load_chunk(nc.sync, x_pool, x_rows, chunks[0])}
         warm = consts.tile([P, 1], F32)
         nc.vector.memset(warm[:], 0.0)
         nc.scalar.activation(out=warm[:], in_=warm[:], func=TANH)
-        w_words, w_scales = load_weights(
-            nc,
-            consts,
-            [(w_theta_words, w_theta_scales, 0, 128), (w_phi_words, w_phi_scales, 128, 128), (w_g_words, w_g_scales, 256, 256)],
-        )
-        for i in range(1, AHEAD):
-            raws[i] = load_chunk(nc, x_pool, x_rows, chunks[i])
+        raws[1] = load_chunk(nc.gpsimd, x_pool, x_rows, chunks[1])
+        theta_bias = load_theta_bias(nc, consts, b_theta)
+        w_words = consts.tile([P, PASSES, C_ALL], U32, align_bytes=64)
+        w_scales = consts.tile([P, PASSES, C_ALL], U8, align_bytes=64)
+        nc.vector.memset(w_scales[:].bitcast(I32), 0)
+        load_scales(nc, w_scales, w_phi_scales, slice(128, 256))
+        load_words(nc, w_words, w_phi_words, slice(128, 256))
+        load_words(nc, w_words, w_g_words, slice(256, 512))
+        load_scales(nc, w_scales, w_g_scales, slice(256, 512))
+        load_words(nc, w_words, w_theta_words, slice(0, 128))
+        load_scales(nc, w_scales, w_theta_scales, slice(0, 128))
+        for i in range(2, AHEAD):
+            raws[i] = load_chunk(nc.sync, x_pool, x_rows, chunks[i])
         identity = consts.tile([P, P], F32)
         make_identity(nc, identity[:])
-        theta_bias = load_theta_bias(nc, consts, psum_turned, identity, b_theta)
         bias_rows = load_bias_rows(nc, consts, b_phi, b_g)
         ones = consts.tile([P, P], BF16)
         nc.vector.memset(ones[:], 1.0)
@@ -309,7 +304,7 @@ def tile_selfattention3d_pb_t_kernel(
             last_chunk = i == len(chunks) - 1
             quantised = quantise(nc, codes_pool, grouped)
             if i + AHEAD < len(chunks):
-                raws[i + AHEAD] = load_chunk(nc, x_pool, x_rows, chunks[i + AHEAD])
+                raws[i + AHEAD] = load_chunk(nc.sync, x_pool, x_rows, chunks[i + AHEAD])
             if not last_chunk:
                 grouped = []
                 for g in range(PASSES):

@@ -38,10 +38,9 @@ THETA_RUN = LOAD // P
 AHEAD = 4
 
 S_LOCATIONS = 448
-V_LOCATIONS = 288
 G_LOCATIONS = 288
 G_OVERLAP = 4
-FIRST_S_LOCATIONS = 344
+FIRST_S_LOCATIONS = 176
 
 FLOPS = 2 * BATCH * LOCATIONS * CHANNELS * C_ALL
 
@@ -78,30 +77,30 @@ def load_bias_rows(nc, consts, b_phi, b_g):
 
 def load_chunk(queue, x_pool, x_rows, chunk):
     b, h = chunk
-    raws = []
+    raw = x_pool.tile([P, PASSES, PACK, CHUNK], BF16)
     for g in range(PASSES):
-        raw = x_pool.tile([P, PACK, CHUNK], BF16)
         queue.dma_start(
-            out=raw[:],
+            out=raw[:, g],
             in_=x_rows[b, g * K_PASS : (g + 1) * K_PASS, h * CHUNK : (h + 1) * CHUNK].rearrange(
                 "(p t) w -> p t w", t=PACK
             ),
         )
-        raws.append(raw)
-    return raws
+    return raw
 
 
-def regroup(engine_copy, grouped, raw, first, count):
-    src = raw[:].rearrange("p t (c i) -> p c t i", i=4)
-    dst = grouped[:].rearrange("p (c i) t -> p c t i", i=4)
-    engine_copy(out=dst[:, first // 4 : (first + count) // 4], in_=src[:, first // 4 : (first + count) // 4])
+def regroup(engine_copy, grouped, raw, load, passes, first, count):
+    at = load * LOAD + first
+    engine_copy(
+        out=grouped[:, load, passes, first : first + count, :].rearrange("p g (c i) t -> p g c t i", i=4),
+        in_=raw[:, passes, :, at : at + count].rearrange("p g t (c i) -> p g c t i", i=4),
+    )
 
 
 def regroup_on_gpsimd(nc, grouped, raw):
-    first = CHUNK - G_LOCATIONS - G_OVERLAP
+    first = LOAD - G_LOCATIONS - G_OVERLAP
     nc.gpsimd.tensor_scalar(
-        out=grouped[:, first:, :],
-        in0=raw[:, :, first:].rearrange("p t w -> p w t"),
+        out=grouped[:, 1, :, first:, :],
+        in0=raw[:, :, :, LOAD + first :].rearrange("p g t w -> p g w t"),
         scalar1=1.0,
         scalar2=0.0,
         op0=MULT,
@@ -109,35 +108,25 @@ def regroup_on_gpsimd(nc, grouped, raw):
     )
 
 
-def quantise(nc, codes_pool, grouped):
-    quantised = []
-    for g in range(PASSES):
-        codes = codes_pool.tile([P, CHUNK], U32, align_bytes=64)
-        scales = codes_pool.tile([P, CHUNK], U8, align_bytes=64)
-        quantised.append((codes, scales))
-    for first in range(0, CHUNK, LOAD):
-        for g in range(PASSES):
-            codes, scales = quantised[g]
-            nc.vector.quantize_mx(
-                out=codes[:, first : first + LOAD].bitcast(FP8X4),
-                scales=scales[:, first : first + LOAD],
-                in_=grouped[g][:, first : first + LOAD, :].rearrange("p w t -> p (w t)"),
-            )
-    return quantised
+def quantise(nc, codes, scales, grouped, load):
+    nc.vector.quantize_mx(
+        out=codes[:, load].rearrange("p g w -> p (g w)").bitcast(FP8X4),
+        scales=scales[:, load].rearrange("p g w -> p (g w)"),
+        in_=grouped[:, load].rearrange("p g w t -> p (g w t)"),
+    )
 
 
 def multiply(nc, psum_sums, quantised, w_words, w_scales, channel_tile, load):
     w_cols = slice(channel_tile * P, (channel_tile + 1) * P)
-    x_cols = slice(load * LOAD, (load + 1) * LOAD)
-    sums = psum_sums.tile([P, LOAD], F32)
+    sums = psum_sums.tile([P, LOAD], F32, tag="sums")
+    codes, scales = quantised
     for g in range(PASSES):
-        codes, scales = quantised[g]
         nc.tensor.matmul_mx(
             out=sums[:],
             lhsT=w_words[:, g, w_cols].bitcast(FP8X4),
             lhsT_scale=w_scales[:, g, w_cols],
-            rhs=codes[:, x_cols].bitcast(FP8X4),
-            rhs_scale=scales[:, x_cols],
+            rhs=codes[:, load, g, :].bitcast(FP8X4),
+            rhs_scale=scales[:, load, g, :],
             start=(g == 0),
             stop=(g == PASSES - 1),
         )
@@ -164,29 +153,34 @@ def products(nc, psum_sums, work, quantised, w_words, w_scales, theta_bias, pool
     return theta_by_channel
 
 
-def open_with_biases(nc, psum_turned, ones, bias_rows, groups):
-    phi_turned = psum_turned.tile([P, LOADS, P], F32)
-    g_turned = psum_turned.tile([P, LOADS, 2, P], F32)
+def open_with_biases(nc, phi_bank, g_bank, ones, bias_rows, groups):
+    phi_pool, phi_tag = phi_bank
+    g_pool, g_tag = g_bank
+    phi_turned = phi_pool.tile([P, LOADS, P], F32, tag=phi_tag)
+    g_turned = g_pool.tile([P, LOADS, 2, P], F32, tag=g_tag)
     nc.tensor.matmul(out=phi_turned[:, :groups], lhsT=ones[:], rhs=bias_rows[:, 0, : groups * P], start=True, stop=False)
     nc.tensor.matmul(out=g_turned[:, :groups], lhsT=ones[:], rhs=bias_rows[:, 1, : groups * 2 * P], start=True, stop=False)
     return phi_turned, g_turned
 
 
-def turn_pooled(nc, results, identity, turned, pooled, first, groups, g_copy, phi_rows, g_rows):
+def turn_pooled(nc, identity, turned, pooled, first, groups):
     phi_turned, g_turned = turned
     for t in range(groups):
         cols = slice(first + t * P, first + (t + 1) * P)
+        last_group = t == groups - 1
         nc.tensor.matmul(
             out=phi_turned[:, t, :], lhsT=pooled[:, 0, cols], rhs=identity[:], is_transpose=True,
-            start=False, stop=(t == groups - 1),
+            start=False, stop=last_group,
         )
-    for t in range(groups):
-        cols = slice(first + t * P, first + (t + 1) * P)
         for half_of_g in range(2):
             nc.tensor.matmul(
                 out=g_turned[:, t, half_of_g, :], lhsT=pooled[:, 1 + half_of_g, cols], rhs=identity[:], is_transpose=True,
-                start=False, stop=(t == groups - 1 and half_of_g == 1),
+                start=False, stop=(last_group and half_of_g == 1),
             )
+
+
+def store_pooled(nc, results, turned, groups, g_copy, phi_rows, g_rows):
+    phi_turned, g_turned = turned
     phi = results.tile([P, LOADS, P], F32)
     g_out = results.tile([P, LOADS, 2, P], F32)
     nc.scalar.activation(out=phi[:, :groups], in_=phi_turned[:, :groups], func=TANH)
@@ -197,10 +191,14 @@ def turn_pooled(nc, results, identity, turned, pooled, first, groups, g_copy, ph
     )
 
 
-def turn_theta(nc, results, psum_theta, identity, theta_by_channel, theta_rows):
+def turn_theta(nc, psum_theta, identity, theta_by_channel):
     theta_turned = psum_theta.tile([P, THETA_RUN, P], F32)
     for t in range(THETA_RUN):
         nc.tensor.transpose(theta_turned[:, t, :], theta_by_channel[:, t, :], identity[:])
+    return theta_turned
+
+
+def store_theta(nc, results, theta_turned, theta_rows):
     theta = results.tile([P, THETA_RUN, P], F32)
     nc.scalar.copy(out=theta[:], in_=theta_turned[:])
     nc.sync.dma_start(
@@ -229,9 +227,9 @@ def tile_selfattention3d_pb_t_kernel(
 
     with ExitStack() as ctx:
         consts = ctx.enter_context(tc.tile_pool(name="consts", bufs=1))
-        x_pool = ctx.enter_context(tc.tile_pool(name="x", bufs=AHEAD * PASSES))
-        grouped_pool = ctx.enter_context(tc.tile_pool(name="grouped", bufs=2 * PASSES))
-        codes_pool = ctx.enter_context(tc.tile_pool(name="codes", bufs=2 * PASSES))
+        x_pool = ctx.enter_context(tc.tile_pool(name="x", bufs=AHEAD))
+        grouped_pool = ctx.enter_context(tc.tile_pool(name="grouped", bufs=2))
+        codes_pool = ctx.enter_context(tc.tile_pool(name="codes", bufs=2))
         work = ctx.enter_context(tc.tile_pool(name="work", bufs=5))
         results = ctx.enter_context(tc.tile_pool(name="results", bufs=3))
         psum_sums = ctx.enter_context(tc.psum_pool(name="psum_sums", bufs=4))
@@ -263,66 +261,86 @@ def tile_selfattention3d_pb_t_kernel(
         ones = consts.tile([P, P], BF16)
         nc.vector.memset(ones[:], 1.0)
 
-        def finish(chunk, thetas, pooled, by_load):
+        phi_bank = (psum_turned, "phi_turned")
+        g_bank = (psum_turned, "g_turned")
+
+        def theta_rows(chunk, load):
             b, h = chunk
-            theta_rows = [out_0[b, h * CHUNK + load * LOAD : h * CHUNK + (load + 1) * LOAD, :] for load in range(LOADS)]
-            if by_load:
-                for load in range(LOADS):
-                    rows = slice(h * POOLED_CHUNK + load * POOLED_LOAD, h * POOLED_CHUNK + (load + 1) * POOLED_LOAD)
-                    if load == 0:
-                        turned = open_with_biases(nc, psum_turned, ones, bias_rows, 1)
-                    turn_theta(nc, results, psum_theta, identity, thetas[load], theta_rows[load])
-                    if load > 0:
-                        turned = open_with_biases(nc, psum_turned, ones, bias_rows, 1)
-                    turn_pooled(
-                        nc, results, identity, turned, pooled, load * POOLED_LOAD, 1, nc.vector.tensor_copy,
-                        out_1[b, rows, :], out_2[b, rows, :],
-                    )
-            else:
-                rows = slice(h * POOLED_CHUNK, (h + 1) * POOLED_CHUNK)
-                turned = open_with_biases(nc, psum_turned, ones, bias_rows, LOADS)
-                for load in range(LOADS):
-                    turn_theta(nc, results, psum_theta, identity, thetas[load], theta_rows[load])
-                turn_pooled(
-                    nc, results, identity, turned, pooled, 0, LOADS, nc.scalar.copy, out_1[b, rows, :], out_2[b, rows, :]
-                )
+            return out_0[b, h * CHUNK + load * LOAD : h * CHUNK + (load + 1) * LOAD, :]
+
+        def pooled_rows(chunk, first, count):
+            b, h = chunk
+            rows = slice(h * POOLED_CHUNK + first, h * POOLED_CHUNK + first + count)
+            return out_1[b, rows, :], out_2[b, rows, :]
 
         ctx.enter_context(
             tc.manual_schedule(
                 engines={mybir.EngineType.PE, mybir.EngineType.DVE, mybir.EngineType.Activation, mybir.EngineType.Pool}
             )
         )
-        grouped = []
-        for g in range(PASSES):
-            grouped_g = grouped_pool.tile([P, CHUNK, PACK], BF16, align_bytes=64, tag="grouped")
-            regroup(nc.scalar.copy, grouped_g, raws[0][g], 0, FIRST_S_LOCATIONS)
-            regroup(nc.vector.tensor_copy, grouped_g, raws[0][g], FIRST_S_LOCATIONS, CHUNK - FIRST_S_LOCATIONS)
-            grouped.append(grouped_g)
+        def new_grouped():
+            tile = grouped_pool.tile([P, LOADS, PASSES, LOAD, PACK], BF16, align_bytes=64, tag="grouped")
+            return tile
 
-        waiting = None
+        def new_quantised():
+            codes = codes_pool.tile([P, LOADS, PASSES, LOAD], U32, align_bytes=64)
+            scales = codes_pool.tile([P, LOADS, PASSES, LOAD], U8, align_bytes=64)
+            return codes, scales
+
+        grouped = new_grouped()
+        quantised = new_quantised()
+        for g, load in ((0, 0), (0, 1), (1, 0), (1, 1)):
+            only_g = slice(g, g + 1)
+            regroup(nc.scalar.copy, grouped, raws[0], load, only_g, 0, FIRST_S_LOCATIONS)
+            regroup(nc.vector.tensor_copy, grouped, raws[0], load, only_g, FIRST_S_LOCATIONS, LOAD - FIRST_S_LOCATIONS)
+            if g == 1:
+                quantise(nc, *quantised, grouped, load)
+
         for i, chunk in enumerate(chunks):
             last_chunk = i == len(chunks) - 1
-            quantised = quantise(nc, codes_pool, grouped)
+            if i > 0:
+                quantised = new_quantised()
+                for load in range(LOADS):
+                    quantise(nc, *quantised, grouped, load)
             if i + AHEAD < len(chunks):
                 raws[i + AHEAD] = load_chunk(nc.sync, x_pool, x_rows, chunks[i + AHEAD])
             if not last_chunk:
-                grouped = []
-                for g in range(PASSES):
-                    grouped_g = grouped_pool.tile([P, CHUNK, PACK], BF16, align_bytes=64, tag="grouped")
-                    regroup(nc.vector.tensor_copy, grouped_g, raws[i + 1][g], S_LOCATIONS, V_LOCATIONS)
-                    grouped.append(grouped_g)
-                for g in reversed(range(PASSES)):
-                    regroup_on_gpsimd(nc, grouped[g], raws[i + 1][g])
+                both = slice(0, PASSES)
+                grouped = new_grouped()
+                raw = raws[i + 1]
+                regroup(nc.vector.tensor_copy, grouped, raw, 0, both, S_LOCATIONS, LOAD - S_LOCATIONS)
+                regroup(nc.vector.tensor_copy, grouped, raw, 1, both, 0, LOAD - G_LOCATIONS)
+                regroup_on_gpsimd(nc, grouped, raw)
+                regroup(nc.scalar.copy, grouped, raw, 0, slice(0, 1), 0, S_LOCATIONS)
+            if i > 0:
+                store_theta(nc, results, theta_turned, theta_rows(chunks[i - 1], 0))
+                store_pooled(nc, results, turned, LOADS, nc.scalar.copy, *pooled_rows(chunks[i - 1], 0, POOLED_CHUNK))
 
             pooled = work.tile([P, len(POOLED_TILES), POOLED_CHUNK], F32)
-            thetas = []
-            for load in range(LOADS):
-                if not last_chunk:
-                    regroup(nc.scalar.copy, grouped[load], raws[i + 1][load], 0, S_LOCATIONS)
-                thetas.append(products(nc, psum_sums, work, quantised, w_words, w_scales, theta_bias, pooled, load))
-                if last_chunk and load == 0:
-                    finish(waiting[0], waiting[1], waiting[2], False)
-            if waiting is not None and not last_chunk:
-                finish(waiting[0], waiting[1], waiting[2], False)
-            waiting = (chunk, thetas, pooled)
-        finish(waiting[0], waiting[1], waiting[2], True)
+            theta_first = products(nc, psum_sums, work, quantised, w_words, w_scales, theta_bias, pooled, 0)
+            if i > 0:
+                theta_turned = turn_theta(nc, psum_theta, identity, theta_second)
+            if not last_chunk:
+                regroup(nc.scalar.copy, grouped, raw, 0, slice(1, 2), 0, S_LOCATIONS)
+            else:
+                store_theta(nc, results, theta_turned, theta_rows(chunks[i - 1], 1))
+            theta_second = products(nc, psum_sums, work, quantised, w_words, w_scales, theta_bias, pooled, 1)
+            if not last_chunk:
+                if i > 0:
+                    store_theta(nc, results, theta_turned, theta_rows(chunks[i - 1], 1))
+                turned = open_with_biases(nc, phi_bank, g_bank, ones, bias_rows, LOADS)
+                theta_turned = turn_theta(nc, psum_theta, identity, theta_first)
+                turn_pooled(nc, identity, turned, pooled, 0, LOADS)
+
+        sums_bank = (psum_sums, "sums")
+        turned_first = open_with_biases(nc, phi_bank, g_bank, ones, bias_rows, 1)
+        turned_second = open_with_biases(nc, sums_bank, sums_bank, ones, bias_rows, 1)
+        theta_turned_first = turn_theta(nc, psum_theta, identity, theta_first)
+        turn_pooled(nc, identity, turned_first, pooled, 0, 1)
+        turn_pooled(nc, identity, turned_second, pooled, POOLED_LOAD, 1)
+        theta_turned_second = turn_theta(nc, psum_theta, identity, theta_second)
+        chunk = chunks[-1]
+        store_theta(nc, results, theta_turned_first, theta_rows(chunk, 0))
+        store_pooled(nc, results, turned_first, 1, nc.vector.tensor_copy, *pooled_rows(chunk, 0, POOLED_LOAD))
+        store_pooled(nc, results, turned_second, 1, nc.vector.tensor_copy, *pooled_rows(chunk, POOLED_LOAD, POOLED_LOAD))
+        store_theta(nc, results, theta_turned_second, theta_rows(chunk, 1))

@@ -35,6 +35,7 @@ CHUNK = LOADS * LOAD
 POOLED_CHUNK = CHUNK // 4
 CHUNKS = LOCATIONS // CHUNK
 THETA_RUN = LOAD // P
+RUN = 8
 AHEAD = 4
 
 S_LOCATIONS = 448
@@ -91,8 +92,8 @@ def load_chunk(queue, x_pool, x_rows, chunk):
 def regroup(engine_copy, grouped, raw, load, passes, first, count):
     at = load * LOAD + first
     engine_copy(
-        out=grouped[:, load, passes, first : first + count, :].rearrange("p g (c i) t -> p g c t i", i=4),
-        in_=raw[:, passes, :, at : at + count].rearrange("p g t (c i) -> p g c t i", i=4),
+        out=grouped[:, load, passes, first : first + count, :].rearrange("p g (c i) t -> p g c t i", i=RUN),
+        in_=raw[:, passes, :, at : at + count].rearrange("p g t (c i) -> p g c t i", i=RUN),
     )
 
 

@@ -39,7 +39,7 @@ RUN = 8
 AHEAD = 4
 
 S_LOCATIONS = 448
-G_LOCATIONS = 288
+G_LOCATIONS = 320
 G_OVERLAP = 4
 FIRST_S_LOCATIONS = 176
 
@@ -313,6 +313,8 @@ def tile_selfattention3d_pb_t_kernel(
                 regroup(nc.vector.tensor_copy, grouped, raw, 1, both, 0, LOAD - G_LOCATIONS)
                 regroup_on_gpsimd(nc, grouped, raw)
                 regroup(nc.scalar.copy, grouped, raw, 0, slice(0, 1), 0, S_LOCATIONS)
+                if i == 0:
+                    regroup(nc.scalar.copy, grouped, raw, 0, slice(1, 2), 0, S_LOCATIONS)
             if i > 0:
                 store_theta(nc, results, theta_turned, theta_rows(chunks[i - 1], 0))
                 store_pooled(nc, results, turned, LOADS, nc.scalar.copy, *pooled_rows(chunks[i - 1], 0, POOLED_CHUNK))
@@ -321,9 +323,9 @@ def tile_selfattention3d_pb_t_kernel(
             theta_first = products(nc, psum_sums, work, quantised, w_words, w_scales, theta_bias, pooled, 0)
             if i > 0:
                 theta_turned = turn_theta(nc, psum_theta, identity, theta_second)
-            if not last_chunk:
+            if 0 < i and not last_chunk:
                 regroup(nc.scalar.copy, grouped, raw, 0, slice(1, 2), 0, S_LOCATIONS)
-            else:
+            if last_chunk:
                 store_theta(nc, results, theta_turned, theta_rows(chunks[i - 1], 1))
             theta_second = products(nc, psum_sums, work, quantised, w_words, w_scales, theta_bias, pooled, 1)
             if not last_chunk:

@@ -39,7 +39,7 @@ RUN = 8
 AHEAD = 4
 
 S_LOCATIONS = 448
-G_LOCATIONS = 320
+G_LOCATIONS = 288
 G_OVERLAP = 4
 FIRST_S_LOCATIONS = 176
 

@@ -76,16 +76,20 @@ def load_bias_rows(nc, consts, b_phi, b_g):
     return bias_rows
 
 
-def load_chunk(queue, x_pool, x_rows, chunk):
+def load_locations(nc, x_rows, chunk, raw, g, first, count):
     b, h = chunk
+    nc.sync.dma_start(
+        out=raw[:, g, :, first : first + count],
+        in_=x_rows[b, g * K_PASS : (g + 1) * K_PASS, h * CHUNK + first : h * CHUNK + first + count].rearrange(
+            "(p t) w -> p t w", t=PACK
+        ),
+    )
+
+
+def load_chunk(nc, x_pool, x_rows, chunk):
     raw = x_pool.tile([P, PASSES, PACK, CHUNK], BF16)
     for g in range(PASSES):
-        queue.dma_start(
-            out=raw[:, g],
-            in_=x_rows[b, g * K_PASS : (g + 1) * K_PASS, h * CHUNK : (h + 1) * CHUNK].rearrange(
-                "(p t) w -> p t w", t=PACK
-            ),
-        )
+        load_locations(nc, x_rows, chunk, raw, g, 0, CHUNK)
     return raw
 
 
@@ -97,11 +101,11 @@ def regroup(engine_copy, grouped, raw, load, passes, first, count):
     )
 
 
-def regroup_on_gpsimd(nc, grouped, raw):
-    first = LOAD - G_LOCATIONS - G_OVERLAP
+def regroup_on_gpsimd(nc, grouped, raw, passes, overlap):
+    first = LOAD - G_LOCATIONS - overlap
     nc.gpsimd.tensor_scalar(
-        out=grouped[:, 1, :, first:, :],
-        in0=raw[:, :, :, LOAD + first :].rearrange("p g t w -> p g w t"),
+        out=grouped[:, 1, passes, first:, :],
+        in0=raw[:, passes, :, LOAD + first :].rearrange("p g t w -> p g w t"),
         scalar1=1.0,
         scalar2=0.0,
         op0=MULT,
@@ -199,9 +203,9 @@ def turn_theta(nc, psum_theta, identity, theta_by_channel):
     return theta_turned
 
 
-def store_theta(nc, results, theta_turned, theta_rows):
+def store_theta(nc, results, theta_turned, theta_copy, theta_rows):
     theta = results.tile([P, THETA_RUN, P], F32)
-    nc.scalar.copy(out=theta[:], in_=theta_turned[:])
+    theta_copy(out=theta[:], in_=theta_turned[:])
     nc.sync.dma_start(
         out=theta_rows.rearrange("(p t) c -> p (t c)", t=THETA_RUN), in_=theta[:].rearrange("p t c -> p (t c)")
     )
@@ -232,30 +236,38 @@ def tile_selfattention3d_pb_t_kernel(
         grouped_pool = ctx.enter_context(tc.tile_pool(name="grouped", bufs=2))
         codes_pool = ctx.enter_context(tc.tile_pool(name="codes", bufs=2))
         work = ctx.enter_context(tc.tile_pool(name="work", bufs=5))
-        results = ctx.enter_context(tc.tile_pool(name="results", bufs=3))
+        results = ctx.enter_context(tc.tile_pool(name="results", bufs=8))
         psum_sums = ctx.enter_context(tc.psum_pool(name="psum_sums", bufs=4))
         psum_theta = ctx.enter_context(tc.psum_pool(name="psum_theta", bufs=2))
         psum_turned = ctx.enter_context(tc.psum_pool(name="psum_turned", bufs=1))
 
         chunks = [(b, h) for b in range(BATCH) for h in range(CHUNKS)]
 
-        raws = {0: load_chunk(nc.sync, x_pool, x_rows, chunks[0])}
+        raw_first = x_pool.tile([P, PASSES, PACK, CHUNK], BF16, tag="raw")
+        raws = {0: raw_first}
+        for g in range(PASSES):
+            load_locations(nc, x_rows, chunks[0], raw_first, g, 0, LOAD)
         warm = consts.tile([P, 1], F32)
         nc.vector.memset(warm[:], 0.0)
         nc.scalar.activation(out=warm[:], in_=warm[:], func=TANH)
-        raws[1] = load_chunk(nc.gpsimd, x_pool, x_rows, chunks[1])
-        theta_bias = load_theta_bias(nc, consts, b_theta)
         w_words = consts.tile([P, PASSES, C_ALL], U32, align_bytes=64)
         w_scales = consts.tile([P, PASSES, C_ALL], U8, align_bytes=64)
         nc.vector.memset(w_scales[:].bitcast(I32), 0)
-        load_scales(nc, w_scales, w_phi_scales, slice(128, 256))
         load_words(nc, w_words, w_phi_words, slice(128, 256))
+        load_scales(nc, w_scales, w_phi_scales, slice(128, 256))
+        for g in range(PASSES):
+            load_locations(nc, x_rows, chunks[0], raw_first, g, LOAD, LOAD)
         load_words(nc, w_words, w_g_words, slice(256, 512))
         load_scales(nc, w_scales, w_g_scales, slice(256, 512))
         load_words(nc, w_words, w_theta_words, slice(0, 128))
+        raw_second = x_pool.tile([P, PASSES, PACK, CHUNK], BF16, tag="raw")
+        raws[1] = raw_second
+        load_locations(nc, x_rows, chunks[1], raw_second, 0, 0, CHUNK)
         load_scales(nc, w_scales, w_theta_scales, slice(0, 128))
+        load_locations(nc, x_rows, chunks[1], raw_second, 1, 0, CHUNK)
+        theta_bias = load_theta_bias(nc, consts, b_theta)
         for i in range(2, AHEAD):
-            raws[i] = load_chunk(nc.sync, x_pool, x_rows, chunks[i])
+            raws[i] = load_chunk(nc, x_pool, x_rows, chunks[i])
         identity = consts.tile([P, P], F32)
         make_identity(nc, identity[:])
         bias_rows = load_bias_rows(nc, consts, b_phi, b_g)
@@ -290,12 +302,12 @@ def tile_selfattention3d_pb_t_kernel(
 
         grouped = new_grouped()
         quantised = new_quantised()
-        for g, load in ((0, 0), (0, 1), (1, 0), (1, 1)):
-            only_g = slice(g, g + 1)
-            regroup(nc.scalar.copy, grouped, raws[0], load, only_g, 0, FIRST_S_LOCATIONS)
-            regroup(nc.vector.tensor_copy, grouped, raws[0], load, only_g, FIRST_S_LOCATIONS, LOAD - FIRST_S_LOCATIONS)
-            if g == 1:
-                quantise(nc, *quantised, grouped, load)
+        for load in range(LOADS):
+            for g in range(PASSES):
+                only_g = slice(g, g + 1)
+                regroup(nc.scalar.copy, grouped, raw_first, load, only_g, 0, FIRST_S_LOCATIONS)
+                regroup(nc.vector.tensor_copy, grouped, raw_first, load, only_g, FIRST_S_LOCATIONS, LOAD - FIRST_S_LOCATIONS)
+            quantise(nc, *quantised, grouped, load)
 
         for i, chunk in enumerate(chunks):
             last_chunk = i == len(chunks) - 1
@@ -304,36 +316,40 @@ def tile_selfattention3d_pb_t_kernel(
                 for load in range(LOADS):
                     quantise(nc, *quantised, grouped, load)
             if i + AHEAD < len(chunks):
-                raws[i + AHEAD] = load_chunk(nc.sync, x_pool, x_rows, chunks[i + AHEAD])
+                raws[i + AHEAD] = load_chunk(nc, x_pool, x_rows, chunks[i + AHEAD])
+            pooled = work.tile([P, len(POOLED_TILES), POOLED_CHUNK], F32)
+            if not last_chunk:
+                grouped_next = new_grouped()
+                raw = raws[i + 1]
+                regroup(nc.scalar.copy, grouped_next, raw, 0, slice(0, 1), 0, S_LOCATIONS)
+            if i == 0:
+                regroup(nc.scalar.copy, grouped_next, raw, 0, slice(1, 2), 0, S_LOCATIONS)
+                regroup_on_gpsimd(nc, grouped_next, raw, slice(0, 1), 0)
+                theta_first = products(nc, psum_sums, work, quantised, w_words, w_scales, theta_bias, pooled, 0)
             if not last_chunk:
                 both = slice(0, PASSES)
-                grouped = new_grouped()
-                raw = raws[i + 1]
-                regroup(nc.vector.tensor_copy, grouped, raw, 0, both, S_LOCATIONS, LOAD - S_LOCATIONS)
-                regroup(nc.vector.tensor_copy, grouped, raw, 1, both, 0, LOAD - G_LOCATIONS)
-                regroup_on_gpsimd(nc, grouped, raw)
-                regroup(nc.scalar.copy, grouped, raw, 0, slice(0, 1), 0, S_LOCATIONS)
-                if i == 0:
-                    regroup(nc.scalar.copy, grouped, raw, 0, slice(1, 2), 0, S_LOCATIONS)
+                regroup(nc.vector.tensor_copy, grouped_next, raw, 0, both, S_LOCATIONS, LOAD - S_LOCATIONS)
+                regroup(nc.vector.tensor_copy, grouped_next, raw, 1, both, 0, LOAD - G_LOCATIONS)
+                regroup_on_gpsimd(nc, grouped_next, raw, slice(1, 2) if i == 0 else both, G_OVERLAP)
             if i > 0:
-                store_theta(nc, results, theta_turned, theta_rows(chunks[i - 1], 0))
+                store_theta(nc, results, theta_turned, nc.scalar.copy, theta_rows(chunks[i - 1], 0))
                 store_pooled(nc, results, turned, LOADS, nc.scalar.copy, *pooled_rows(chunks[i - 1], 0, POOLED_CHUNK))
-
-            pooled = work.tile([P, len(POOLED_TILES), POOLED_CHUNK], F32)
-            theta_first = products(nc, psum_sums, work, quantised, w_words, w_scales, theta_bias, pooled, 0)
-            if i > 0:
-                theta_turned = turn_theta(nc, psum_theta, identity, theta_second)
-            if 0 < i and not last_chunk:
-                regroup(nc.scalar.copy, grouped, raw, 0, slice(1, 2), 0, S_LOCATIONS)
+                theta_first = products(nc, psum_sums, work, quantised, w_words, w_scales, theta_bias, pooled, 0)
             if last_chunk:
-                store_theta(nc, results, theta_turned, theta_rows(chunks[i - 1], 1))
+                store_theta(nc, results, theta_turned_left, nc.scalar.copy, theta_rows(chunks[i - 1], 1))
+            elif i > 0:
+                theta_turned = turn_theta(nc, psum_theta, identity, theta_second)
+                regroup(nc.scalar.copy, grouped_next, raw, 0, slice(1, 2), 0, S_LOCATIONS)
             theta_second = products(nc, psum_sums, work, quantised, w_words, w_scales, theta_bias, pooled, 1)
             if not last_chunk:
                 if i > 0:
-                    store_theta(nc, results, theta_turned, theta_rows(chunks[i - 1], 1))
+                    store_theta(nc, results, theta_turned, nc.scalar.copy, theta_rows(chunks[i - 1], 1))
                 turned = open_with_biases(nc, phi_bank, g_bank, ones, bias_rows, LOADS)
                 theta_turned = turn_theta(nc, psum_theta, identity, theta_first)
                 turn_pooled(nc, identity, turned, pooled, 0, LOADS)
+                grouped = grouped_next
+            if i == len(chunks) - 2:
+                theta_turned_left = turn_theta(nc, psum_theta, identity, theta_second)
 
         sums_bank = (psum_sums, "sums")
         turned_first = open_with_biases(nc, phi_bank, g_bank, ones, bias_rows, 1)
@@ -343,7 +359,7 @@ def tile_selfattention3d_pb_t_kernel(
         turn_pooled(nc, identity, turned_second, pooled, POOLED_LOAD, 1)
         theta_turned_second = turn_theta(nc, psum_theta, identity, theta_second)
         chunk = chunks[-1]
-        store_theta(nc, results, theta_turned_first, theta_rows(chunk, 0))
+        store_theta(nc, results, theta_turned_first, nc.vector.tensor_copy, theta_rows(chunk, 0))
         store_pooled(nc, results, turned_first, 1, nc.vector.tensor_copy, *pooled_rows(chunk, 0, POOLED_LOAD))
         store_pooled(nc, results, turned_second, 1, nc.vector.tensor_copy, *pooled_rows(chunk, POOLED_LOAD, POOLED_LOAD))
-        store_theta(nc, results, theta_turned_second, theta_rows(chunk, 1))
+        store_theta(nc, results, theta_turned_second, nc.scalar.copy, theta_rows(chunk, 1))

from contextlib import ExitStack

import concourse.mybir as mybir
from concourse.masks import make_identity

BF16 = mybir.dt.bfloat16
F32 = mybir.dt.float32
I32 = mybir.dt.int32
U32 = mybir.dt.uint32
U8 = mybir.dt.uint8
FP8X4 = mybir.dt.float8_e4m3fn_x4
MAX = mybir.AluOpType.max
MULT = mybir.AluOpType.mult
ADD = mybir.AluOpType.add
TANH = mybir.ActivationFunctionType.Tanh

P = 128
PACK = 4
K_PASS = P * PACK

BATCH = 2
CHANNELS = 1024
PASSES = CHANNELS // K_PASS
LOCATIONS = 16 * 16 * 16
SIDE = 16

C_ALL = 512
THETA = 0
POOLED_TILES = (1, 2, 3)

LOAD = 512
POOLED_LOAD = LOAD // 4
LOADS = 2
CHUNK = LOADS * LOAD
POOLED_CHUNK = CHUNK // 4
CHUNKS = LOCATIONS // CHUNK
THETA_RUN = LOAD // P
RUN = 8
AHEAD = 4

S_LOCATIONS = 448
G_LOCATIONS = 288
G_OVERLAP = 4
FIRST_S_LOCATIONS = 176

FLOPS = 2 * BATCH * LOCATIONS * CHANNELS * C_ALL


def load_words(nc, w_words, words, cols):
    nc.sync.dma_start(
        out=w_words[:, :, cols].bitcast(I32),
        in_=words.rearrange("g p n t -> p g (n t)").bitcast(I32),
    )


def load_scales(nc, w_scales, scales, cols):
    for quadrant in range(4):
        nc.sync.dma_start(
            out=w_scales[32 * quadrant : 32 * quadrant + 4, :, cols].bitcast(I32),
            in_=scales[:, 4 * quadrant : 4 * quadrant + 4, :].rearrange("g r n -> r g n").bitcast(I32),
        )


def load_theta_bias(nc, consts, b_theta):
    theta_bias = consts.tile([P, 1], BF16)
    nc.gpsimd.dma_start(out=theta_bias[:], in_=b_theta.rearrange("(p c) -> p c", c=1))
    return theta_bias


def load_bias_rows(nc, consts, b_phi, b_g):
    bias_rows = consts.tile([P, 2, 4 * P], BF16)
    nc.vector.memset(bias_rows[:], 0.0)
    for t in range(LOADS):
        nc.gpsimd.dma_start(out=bias_rows[0:1, 0, t * P : (t + 1) * P], in_=b_phi.rearrange("(k c) -> k c", k=1))
        nc.gpsimd.dma_start(out=bias_rows[0:1, 1, t * 2 * P : (t + 1) * 2 * P], in_=b_g.rearrange("(k c) -> k c", k=1))
    return bias_rows


def load_locations(nc, x_rows, chunk, raw, g, first, count):
    b, h = chunk
    nc.sync.dma_start(
        out=raw[:, g, :, first : first + count],
        in_=x_rows[b, g * K_PASS : (g + 1) * K_PASS, h * CHUNK + first : h * CHUNK + first + count].rearrange(
            "(p t) w -> p t w", t=PACK
        ),
    )


def load_chunk(nc, x_pool, x_rows, chunk):
    raw = x_pool.tile([P, PASSES, PACK, CHUNK], BF16)
    for g in range(PASSES):
        load_locations(nc, x_rows, chunk, raw, g, 0, CHUNK)
    return raw


def regroup(engine_copy, grouped, raw, load, passes, first, count):
    at = load * LOAD + first
    engine_copy(
        out=grouped[:, load, passes, first : first + count, :].rearrange("p g (c i) t -> p g c t i", i=RUN),
        in_=raw[:, passes, :, at : at + count].rearrange("p g t (c i) -> p g c t i", i=RUN),
    )


def regroup_on_gpsimd(nc, grouped, raw, passes, overlap):
    first = LOAD - G_LOCATIONS - overlap
    nc.gpsimd.tensor_scalar(
        out=grouped[:, 1, passes, first:, :],
        in0=raw[:, passes, :, LOAD + first :].rearrange("p g t w -> p g w t"),
        scalar1=1.0,
        scalar2=0.0,
        op0=MULT,
        op1=ADD,
    )


def quantise(nc, codes, scales, grouped, load):
    nc.vector.quantize_mx(
        out=codes[:, load].rearrange("p g w -> p (g w)").bitcast(FP8X4),
        scales=scales[:, load].rearrange("p g w -> p (g w)"),
        in_=grouped[:, load].rearrange("p g w t -> p (g w t)"),
    )


def multiply(nc, psum_sums, quantised, w_words, w_scales, channel_tile, load):
    w_cols = slice(channel_tile * P, (channel_tile + 1) * P)
    sums = psum_sums.tile([P, LOAD], F32, tag="sums")
    codes, scales = quantised
    for g in range(PASSES):
        nc.tensor.matmul_mx(
            out=sums[:],
            lhsT=w_words[:, g, w_cols].bitcast(FP8X4),
            lhsT_scale=w_scales[:, g, w_cols],
            rhs=codes[:, load, g, :].bitcast(FP8X4),
            rhs_scale=scales[:, load, g, :],
            start=(g == 0),
            stop=(g == PASSES - 1),
        )
    return sums


def products(nc, psum_sums, work, quantised, w_words, w_scales, theta_bias, pooled, load):
    for k, channel_tile in enumerate(POOLED_TILES):
        sums = multiply(nc, psum_sums, quantised, w_words, w_scales, channel_tile, load)
        nc.vector.tensor_reduce(
            out=pooled[:, k, load * POOLED_LOAD : (load + 1) * POOLED_LOAD].rearrange("c (pair j) -> c pair j", j=SIDE // 2),
            in_=sums[:].rearrange("c (pair half j side) -> c pair j half side", half=2, j=SIDE // 2, side=2),
            axis=mybir.AxisListType.XY,
            op=MAX,
        )
    sums = multiply(nc, psum_sums, quantised, w_words, w_scales, THETA, load)
    theta_by_channel = work.tile([P, THETA_RUN, P], F32)
    nc.scalar.activation(
        out=theta_by_channel[:],
        in_=sums[:].rearrange("c (p t) -> c t p", t=THETA_RUN),
        func=TANH,
        bias=theta_bias[:],
    )
    return theta_by_channel


def open_with_biases(nc, phi_bank, g_bank, ones, bias_rows, groups):
    phi_pool, phi_tag = phi_bank
    g_pool, g_tag = g_bank
    phi_turned = phi_pool.tile([P, LOADS, P], F32, tag=phi_tag)
    g_turned = g_pool.tile([P, LOADS, 2, P], F32, tag=g_tag)
    nc.tensor.matmul(out=phi_turned[:, :groups], lhsT=ones[:], rhs=bias_rows[:, 0, : groups * P], start=True, stop=False)
    nc.tensor.matmul(out=g_turned[:, :groups], lhsT=ones[:], rhs=bias_rows[:, 1, : groups * 2 * P], start=True, stop=False)
    return phi_turned, g_turned


def turn_pooled(nc, identity, turned, pooled, first, groups):
    phi_turned, g_turned = turned
    for t in range(groups):
        cols = slice(first + t * P, first + (t + 1) * P)
        last_group = t == groups - 1
        nc.tensor.matmul(
            out=phi_turned[:, t, :], lhsT=pooled[:, 0, cols], rhs=identity[:], is_transpose=True,
            start=False, stop=last_group,
        )
        for half_of_g in range(2):
            nc.tensor.matmul(
                out=g_turned[:, t, half_of_g, :], lhsT=pooled[:, 1 + half_of_g, cols], rhs=identity[:], is_transpose=True,
                start=False, stop=(last_group and half_of_g == 1),
            )


def store_pooled(nc, results, turned, groups, g_copy, phi_rows, g_rows):
    phi_turned, g_turned = turned
    phi = results.tile([P, LOADS, P], F32)
    g_out = results.tile([P, LOADS, 2, P], F32)
    nc.scalar.activation(out=phi[:, :groups], in_=phi_turned[:, :groups], func=TANH)
    g_copy(out=g_out[:, :groups], in_=g_turned[:, :groups])
    nc.sync.dma_start(out=phi_rows.rearrange("(t p) c -> p t c", t=groups), in_=phi[:, :groups])
    nc.sync.dma_start(
        out=g_rows.rearrange("(t p) c -> p t c", t=groups), in_=g_out[:, :groups].rearrange("p t k c -> p t (k c)")
    )


def turn_theta(nc, psum_theta, identity, theta_by_channel):
    theta_turned = psum_theta.tile([P, THETA_RUN, P], F32)
    for t in range(THETA_RUN):
        nc.tensor.transpose(theta_turned[:, t, :], theta_by_channel[:, t, :], identity[:])
    return theta_turned


def store_theta(nc, results, theta_turned, theta_copy, theta_rows):
    theta = results.tile([P, THETA_RUN, P], F32)
    theta_copy(out=theta[:], in_=theta_turned[:])
    nc.sync.dma_start(
        out=theta_rows.rearrange("(p t) c -> p (t c)", t=THETA_RUN), in_=theta[:].rearrange("p t c -> p (t c)")
    )


def tile_selfattention3d_pb_t_kernel(
    tc,
    x,
    w_theta_words,
    w_theta_scales,
    b_theta,
    w_phi_words,
    w_phi_scales,
    b_phi,
    w_g_words,
    w_g_scales,
    b_g,
    out_0,
    out_1,
    out_2,
):
    nc = tc.nc
    x_rows = x.rearrange("b c f i j -> b c (f i j)")

    with ExitStack() as ctx:
        consts = ctx.enter_context(tc.tile_pool(name="consts", bufs=1))
        x_pool = ctx.enter_context(tc.tile_pool(name="x", bufs=AHEAD))
        grouped_pool = ctx.enter_context(tc.tile_pool(name="grouped", bufs=2))
        codes_pool = ctx.enter_context(tc.tile_pool(name="codes", bufs=2))
        work = ctx.enter_context(tc.tile_pool(name="work", bufs=5))
        results = ctx.enter_context(tc.tile_pool(name="results", bufs=8))
        psum_sums = ctx.enter_context(tc.psum_pool(name="psum_sums", bufs=4))
        psum_theta = ctx.enter_context(tc.psum_pool(name="psum_theta", bufs=2))
        psum_turned = ctx.enter_context(tc.psum_pool(name="psum_turned", bufs=1))

        chunks = [(b, h) for b in range(BATCH) for h in range(CHUNKS)]

        raw_first = x_pool.tile([P, PASSES, PACK, CHUNK], BF16, tag="raw")
        raws = {0: raw_first}
        for g in range(PASSES):
            load_locations(nc, x_rows, chunks[0], raw_first, g, 0, LOAD)
        warm = consts.tile([P, 1], F32)
        nc.vector.memset(warm[:], 0.0)
        nc.scalar.activation(out=warm[:], in_=warm[:], func=TANH)
        w_words = consts.tile([P, PASSES, C_ALL], U32, align_bytes=64)
        w_scales = consts.tile([P, PASSES, C_ALL], U8, align_bytes=64)
        nc.vector.memset(w_scales[:].bitcast(I32), 0)
        load_words(nc, w_words, w_phi_words, slice(128, 256))
        load_scales(nc, w_scales, w_phi_scales, slice(128, 256))
        for g in range(PASSES):
            load_locations(nc, x_rows, chunks[0], raw_first, g, LOAD, LOAD)
        load_words(nc, w_words, w_g_words, slice(256, 512))
        load_scales(nc, w_scales, w_g_scales, slice(256, 512))
        load_words(nc, w_words, w_theta_words, slice(0, 128))
        raw_second = x_pool.tile([P, PASSES, PACK, CHUNK], BF16, tag="raw")
        raws[1] = raw_second
        load_locations(nc, x_rows, chunks[1], raw_second, 0, 0, CHUNK)
        load_scales(nc, w_scales, w_theta_scales, slice(0, 128))
        load_locations(nc, x_rows, chunks[1], raw_second, 1, 0, CHUNK)
        theta_bias = load_theta_bias(nc, consts, b_theta)
        for i in range(2, AHEAD):
            raws[i] = load_chunk(nc, x_pool, x_rows, chunks[i])
        identity = consts.tile([P, P], F32)
        make_identity(nc, identity[:])
        bias_rows = load_bias_rows(nc, consts, b_phi, b_g)
        ones = consts.tile([P, P], BF16)
        nc.vector.memset(ones[:], 1.0)

        phi_bank = (psum_turned, "phi_turned")
        g_bank = (psum_turned, "g_turned")

        def theta_rows(chunk, load):
            b, h = chunk
            return out_0[b, h * CHUNK + load * LOAD : h * CHUNK + (load + 1) * LOAD, :]

        def pooled_rows(chunk, first, count):
            b, h = chunk
            rows = slice(h * POOLED_CHUNK + first, h * POOLED_CHUNK + first + count)
            return out_1[b, rows, :], out_2[b, rows, :]

        ctx.enter_context(
            tc.manual_schedule(
                engines={mybir.EngineType.PE, mybir.EngineType.DVE, mybir.EngineType.Activation, mybir.EngineType.Pool}
            )
        )
        def new_grouped():
            tile = grouped_pool.tile([P, LOADS, PASSES, LOAD, PACK], BF16, align_bytes=64, tag="grouped")
            return tile

        def new_quantised():
            codes = codes_pool.tile([P, LOADS, PASSES, LOAD], U32, align_bytes=64)
            scales = codes_pool.tile([P, LOADS, PASSES, LOAD], U8, align_bytes=64)
            return codes, scales

        grouped = new_grouped()
        quantised = new_quantised()
        for load in range(LOADS):
            for g in range(PASSES):
                only_g = slice(g, g + 1)
                regroup(nc.scalar.copy, grouped, raw_first, load, only_g, 0, FIRST_S_LOCATIONS)
                regroup(nc.vector.tensor_copy, grouped, raw_first, load, only_g, FIRST_S_LOCATIONS, LOAD - FIRST_S_LOCATIONS)
            quantise(nc, *quantised, grouped, load)

        for i, chunk in enumerate(chunks):
            last_chunk = i == len(chunks) - 1
            if i > 0:
                quantised = new_quantised()
                for load in range(LOADS):
                    quantise(nc, *quantised, grouped, load)
            if i + AHEAD < len(chunks):
                raws[i + AHEAD] = load_chunk(nc, x_pool, x_rows, chunks[i + AHEAD])
            pooled = work.tile([P, len(POOLED_TILES), POOLED_CHUNK], F32)
            if not last_chunk:
                grouped_next = new_grouped()
                raw = raws[i + 1]
                regroup(nc.scalar.copy, grouped_next, raw, 0, slice(0, 1), 0, S_LOCATIONS)
            if i == 0:
                regroup(nc.scalar.copy, grouped_next, raw, 0, slice(1, 2), 0, S_LOCATIONS)
                regroup_on_gpsimd(nc, grouped_next, raw, slice(0, 1), 0)
                theta_first = products(nc, psum_sums, work, quantised, w_words, w_scales, theta_bias, pooled, 0)
            if not last_chunk:
                both = slice(0, PASSES)
                regroup(nc.vector.tensor_copy, grouped_next, raw, 0, both, S_LOCATIONS, LOAD - S_LOCATIONS)
                regroup(nc.vector.tensor_copy, grouped_next, raw, 1, both, 0, LOAD - G_LOCATIONS)
                regroup_on_gpsimd(nc, grouped_next, raw, slice(1, 2) if i == 0 else both, G_OVERLAP)
            if i > 0:
                store_theta(nc, results, theta_turned, nc.scalar.copy, theta_rows(chunks[i - 1], 0))
                store_pooled(nc, results, turned, LOADS, nc.scalar.copy, *pooled_rows(chunks[i - 1], 0, POOLED_CHUNK))
                theta_first = products(nc, psum_sums, work, quantised, w_words, w_scales, theta_bias, pooled, 0)
            if last_chunk:
                store_theta(nc, results, theta_turned_left, nc.scalar.copy, theta_rows(chunks[i - 1], 1))
            elif i > 0:
                theta_turned = turn_theta(nc, psum_theta, identity, theta_second)
                regroup(nc.scalar.copy, grouped_next, raw, 0, slice(1, 2), 0, S_LOCATIONS)
            theta_second = products(nc, psum_sums, work, quantised, w_words, w_scales, theta_bias, pooled, 1)
            if not last_chunk:
                if i > 0:
                    store_theta(nc, results, theta_turned, nc.scalar.copy, theta_rows(chunks[i - 1], 1))
                turned = open_with_biases(nc, phi_bank, g_bank, ones, bias_rows, LOADS)
                theta_turned = turn_theta(nc, psum_theta, identity, theta_first)
                turn_pooled(nc, identity, turned, pooled, 0, LOADS)
                grouped = grouped_next
            if i == len(chunks) - 2:
                theta_turned_left = turn_theta(nc, psum_theta, identity, theta_second)

        sums_bank = (psum_sums, "sums")
        turned_first = open_with_biases(nc, phi_bank, g_bank, ones, bias_rows, 1)
        turned_second = open_with_biases(nc, sums_bank, sums_bank, ones, bias_rows, 1)
        theta_turned_first = turn_theta(nc, psum_theta, identity, theta_first)
        turn_pooled(nc, identity, turned_first, pooled, 0, 1)
        turn_pooled(nc, identity, turned_second, pooled, POOLED_LOAD, 1)
        theta_turned_second = turn_theta(nc, psum_theta, identity, theta_second)
        chunk = chunks[-1]
        store_theta(nc, results, theta_turned_first, nc.vector.tensor_copy, theta_rows(chunk, 0))
        store_pooled(nc, results, turned_first, 1, nc.vector.tensor_copy, *pooled_rows(chunk, 0, POOLED_LOAD))
        store_pooled(nc, results, turned_second, 1, nc.vector.tensor_copy, *pooled_rows(chunk, POOLED_LOAD, POOLED_LOAD))
        store_theta(nc, results, theta_turned_second, nc.scalar.copy, theta_rows(chunk, 1))
